import numpy as np
import ml_dtypes


def mxq(x, axis, fmt="e4m3"):
    dtype, down = {"e4m3": (ml_dtypes.float8_e4m3fn, 7), "e5m2": (ml_dtypes.float8_e5m2, 14)}[fmt]
    v = np.moveaxis(np.asarray(x, np.float32).astype(ml_dtypes.bfloat16).astype(np.float64), axis, -1)
    blocks = v.reshape(v.shape[:-1] + (-1, 32))
    amax = np.abs(blocks).max(-1, keepdims=True)
    byte = np.maximum(np.where(amax > 0, np.frexp(amax)[1] - 1 + 127, 0) - down, 1)
    scale = np.exp2(byte - 127.0)
    codes = (blocks / scale).astype(np.float32).astype(dtype).astype(np.float64)
    return np.moveaxis((codes * scale).reshape(v.shape), -1, axis)


WIDE = False


def mx_kscale(k):
    if not WIDE:
        return np.ones(k)
    levels = np.array([10, -10, 5, -5, 0])
    a = np.random.permutation(np.resize(levels, k // 512 * 4)).reshape(k // 512, 4)
    idx = np.arange(k)
    return np.exp2(a[idx // 512, idx % 128 // 32])


BF16 = ml_dtypes.bfloat16


def bf(x):
    return np.asarray(x, np.float32).astype(BF16)


def f64(x):
    return np.asarray(x).astype(np.float64)


B, I, O, G = 4096, 512, 512, 2
K = I * G


def bspline_basis(d):
    inner = 1.0 - 6.0 * d * d + 6.0 * d * d * d
    outer = 2.0 * (1.0 - d) ** 3
    return np.where(d < 0.5, inner, np.where(d < 1.0, outer, np.zeros_like(d)))


def setup_inputs():
    g = np.linspace(-1.0, 1.0, G)
    s = mx_kscale(I)
    u = s / s.max()
    return {"x_norm": bf(np.tanh(np.random.standard_normal((B, I))) * u),
            "spline_weight": bf(np.random.standard_normal((O, I, G)) / np.sqrt(I)),
            "base_activation": bf(np.random.standard_normal((O, I)) * 4.0 / np.sqrt(I) / u),
            "grid_points": bf(g + 0.1 * (g[1] - g[0]) * np.random.standard_normal(G))}


def reference(x_norm, spline_weight, base_activation, grid_points):
    t = f64(x_norm)
    d = np.abs(t[:, :, None] - f64(grid_points))
    basis = bspline_basis(d)
    spline_out = mxq(basis.reshape(B, K), 1, "e4m3") @ mxq(f64(spline_weight).reshape(O, K), 1, "e4m3").T
    base_out = mxq(t, 1, "e4m3") @ mxq(f64(base_activation), 1, "e4m3").T
    return spline_out + 0.1 * base_out

@@ -1,0 +1,170 @@
+from contextlib import ExitStack
+
+import concourse.mybir as mybir
+from concourse.masks import make_identity
+
+F32 = mybir.dt.float32
+BF16 = mybir.dt.bfloat16
+U32 = mybir.dt.uint32
+U8 = mybir.dt.uint8
+FP8X4 = mybir.dt.float8_e4m3fn_x4
+ALU = mybir.AluOpType
+ACT = mybir.ActivationFunctionType
+
+P = 128
+PACK = 4
+BATCH, FEATURES, OUTPUTS, KNOTS = 4096, 512, 512, 2
+FLOPS = 2 * BATCH * OUTPUTS * (FEATURES * KNOTS + FEATURES)
+
+ROW_TILES = BATCH // P
+PAIR = 2
+PAIR_ROWS = PAIR * P
+ROUNDS = ROW_TILES // PAIR
+GROUPED = PAIR_ROWS * PACK
+HALVES = 2
+
+
+def features_to_partitions(nc, psum, identity, rows, grouped, copy):
+    turned = psum.tile([P, HALVES, PAIR_ROWS], F32, tag="turned")
+    for h in range(HALVES):
+        for t in range(PAIR):
+            nc.tensor.transpose(
+                out=turned[:, h, t * P : (t + 1) * P],
+                in_=rows[:, t, :].bitcast(F32)[:, h * P : (h + 1) * P],
+                identity=identity,
+            )
+    copy(
+        out=grouped.bitcast(F32).rearrange("p (r h) -> p r h", h=HALVES),
+        in_=turned[:].rearrange("p h r -> p r h"),
+    )
+
+
+def tile_advancedkanlayer_pa_t_kernel(tc, x_norm, spline_weight, base_activation, grid_points, out):
+    nc = tc.nc
+    with ExitStack() as stack:
+        consts = stack.enter_context(tc.tile_pool(name="consts", bufs=1))
+        weights = stack.enter_context(tc.tile_pool(name="weights", bufs=1))
+        loads = stack.enter_context(tc.tile_pool(name="loads", bufs=4))
+        from_scalar = stack.enter_context(tc.tile_pool(name="from_scalar", bufs=3))
+        from_vector = stack.enter_context(tc.tile_pool(name="from_vector", bufs=2))
+        operands = stack.enter_context(tc.tile_pool(name="operands", bufs=3))
+        results = stack.enter_context(tc.tile_pool(name="results", bufs=3))
+        turn_psum = stack.enter_context(tc.psum_pool(name="turn_psum", bufs=2))
+        acc_psum = stack.enter_context(tc.psum_pool(name="acc_psum", bufs=3))
+
+        knots = consts.tile([P, KNOTS], BF16)
+        nc.scalar.dma_start(out=knots[:], in_=grid_points.partition_broadcast(P))
+        minus_two_knots = consts.tile([P, KNOTS], F32)
+        nc.vector.tensor_scalar_mul(out=minus_two_knots[:], in0=knots[:], scalar1=-2.0)
+        minus_one = consts.tile([P, 1], F32)
+        nc.vector.memset(minus_one[:], -1.0)
+        identity = consts.tile([P, P], F32)
+        make_identity(nc, identity[:])
+
+        x_view = x_norm.rearrange("(p t) i -> p t i", t=ROW_TILES)
+        out_view = out.rearrange("(p t) o -> p t o", t=ROW_TILES)
+
+        x_rows = {}
+        x_rows[0] = loads.tile([P, PAIR, FEATURES], BF16, name="x_rows", tag="x_rows")
+        nc.sync.dma_start(out=x_rows[0][:], in_=x_view[:, 0:PAIR, :])
+        out_tiles = OUTPUTS // P
+        w_rows = weights.tile([P, out_tiles, FEATURES * KNOTS], BF16)
+        nc.sync.dma_start(out=w_rows[:], in_=spline_weight.rearrange("(c p) i g -> p c (i g)", p=P))
+        a_rows = weights.tile([P, out_tiles, FEATURES], BF16)
+        nc.sync.dma_start(out=a_rows[:], in_=base_activation.rearrange("(c p) i -> p c i", p=P))
+
+        knot_rows = weights.tile([P, KNOTS, out_tiles, FEATURES], BF16)
+        for g in range(KNOTS):
+            nc.vector.tensor_copy(
+                out=knot_rows[:, g],
+                in_=w_rows[:].rearrange("p c (i g) -> p g c i", g=KNOTS)[:, g],
+            )
+
+        def quantise_weight(label, rows):
+            grouped = weights.tile([P, OUTPUTS * PACK], BF16, align_bytes=64, name="%s_grouped" % label)
+            for pair in range(out_tiles // PAIR):
+                features_to_partitions(
+                    nc,
+                    turn_psum,
+                    identity[:],
+                    rows[:, pair * PAIR : (pair + 1) * PAIR, :],
+                    grouped[:, pair * GROUPED : (pair + 1) * GROUPED],
+                    nc.vector.tensor_copy,
+                )
+            codes = weights.tile([P, OUTPUTS], U32, align_bytes=64, name="%s_codes" % label)
+            scales = weights.tile([P, OUTPUTS], U8, align_bytes=64, name="%s_scales" % label)
+            nc.vector.quantize_mx(out=codes[:].bitcast(FP8X4), scales=scales[:], in_=grouped[:])
+            return codes, scales
+
+        knot_weights = [quantise_weight("knot%d" % g, knot_rows[:, g]) for g in range(KNOTS)]
+        base_codes, base_scales = quantise_weight("base", a_rows[:])
+
+        for r in range(ROUNDS):
+            tiles = slice(r * PAIR, (r + 1) * PAIR)
+            if r > 0:
+                x_rows[r] = loads.tile([P, PAIR, FEATURES], BF16, name="x_rows", tag="x_rows")
+                nc.sync.dma_start(out=x_rows[r][:], in_=x_view[:, tiles, :])
+
+            x_grouped = from_scalar.tile([P, GROUPED], BF16, align_bytes=64)
+            features_to_partitions(nc, turn_psum, identity[:], x_rows[r][:], x_grouped[:], nc.scalar.copy)
+            x_codes = operands.tile([P, PAIR_ROWS], U32, align_bytes=64)
+            x_scales = operands.tile([P, PAIR_ROWS], U8, align_bytes=64)
+            nc.vector.quantize_mx(out=x_codes[:].bitcast(FP8X4), scales=x_scales[:], in_=x_grouped[:])
+
+            dist = from_scalar.tile([P, KNOTS, GROUPED], F32)
+            for g in range(KNOTS):
+                nc.scalar.activation(
+                    out=dist[:, g, :], in_=x_grouped[:], func=ACT.Abs, bias=minus_two_knots[:, g : g + 1], scale=2.0
+                )
+            outer_sq = from_scalar.tile([P, KNOTS, GROUPED], F32)
+            nc.scalar.activation(out=outer_sq[:], in_=dist[:], func=ACT.Square, bias=minus_one[:], scale=0.5)
+            inner_sq = from_scalar.tile([P, KNOTS, GROUPED], F32)
+            nc.scalar.activation(out=inner_sq[:], in_=dist[:], func=ACT.Square, bias=minus_one[:], scale=1.0)
+            outer_cube = from_vector.tile([P, KNOTS, GROUPED], F32)
+            nc.vector.scalar_tensor_tensor(
+                out=outer_cube[:], in0=dist[:], scalar=2.0, in1=outer_sq[:], op0=ALU.subtract, op1=ALU.mult
+            )
+            inner_cube = from_vector.tile([P, KNOTS, GROUPED], F32)
+            nc.vector.scalar_tensor_tensor(
+                out=inner_cube[:], in0=dist[:], scalar=1.0, in1=inner_sq[:], op0=ALU.subtract, op1=ALU.mult
+            )
+            signed = from_vector.tile([P, KNOTS, GROUPED], BF16)
+            nc.vector.scalar_tensor_tensor(
+                out=signed[:], in0=inner_cube[:], scalar=0.0, in1=outer_cube[:], op0=ALU.min, op1=ALU.subtract
+            )
+            basis = from_vector.tile([P, KNOTS * GROUPED], BF16, align_bytes=64)
+            nc.vector.tensor_scalar_max(
+                out=basis[:], in0=signed[:].rearrange("p g c -> p (g c)"), scalar1=0.0
+            )
+            basis_codes = operands.tile([P, KNOTS * PAIR_ROWS], U32, align_bytes=64)
+            basis_scales = operands.tile([P, KNOTS * PAIR_ROWS], U8, align_bytes=64)
+            nc.vector.quantize_mx(out=basis_codes[:].bitcast(FP8X4), scales=basis_scales[:], in_=basis[:])
+
+            result = results.tile([P, PAIR, OUTPUTS], F32)
+            for t in range(PAIR):
+                spline_acc = acc_psum.tile([P, OUTPUTS], F32)
+                for g in range(KNOTS):
+                    cols = slice(g * PAIR_ROWS + t * P, g * PAIR_ROWS + (t + 1) * P)
+                    nc.tensor.matmul_mx(
+                        out=spline_acc[:],
+                        lhsT=basis_codes[:, cols].bitcast(FP8X4),
+                        lhsT_scale=basis_scales[:, cols],
+                        rhs=knot_weights[g][0][:].bitcast(FP8X4),
+                        rhs_scale=knot_weights[g][1][:],
+                        start=(g == 0),
+                        stop=(g == KNOTS - 1),
+                    )
+                base_acc = acc_psum.tile([P, OUTPUTS], F32)
+                nc.tensor.matmul_mx(
+                    out=base_acc[:],
+                    lhsT=x_codes[:, t * P : (t + 1) * P].bitcast(FP8X4),
+                    lhsT_scale=x_scales[:, t * P : (t + 1) * P],
+                    rhs=base_codes[:].bitcast(FP8X4),
+                    rhs_scale=base_scales[:],
+                    start=True,
+                    stop=True,
+                )
+                tenth = results.tile([P, OUTPUTS], F32)
+                nc.scalar.activation(out=tenth[:], in_=base_acc[:], func=ACT.Copy, scale=0.1)
+                nc.vector.tensor_tensor(out=result[:, t, :], in0=spline_acc[:], in1=tenth[:], op=ALU.add)
+            nc.sync.dma_start(out=out_view[:, tiles, :], in_=result[:])

@@ -17,6 +17,7 @@ BATCH, FEATURES, OUTPUTS, KNOTS = 4096, 512, 512, 2
 FLOPS = 2 * BATCH * OUTPUTS * (FEATURES * KNOTS + FEATURES)
 
 ROW_TILES = BATCH // P
+OUT_TILES = OUTPUTS // P
 PAIR = 2
 PAIR_ROWS = PAIR * P
 ROUNDS = ROW_TILES // PAIR
@@ -24,8 +25,7 @@ GROUPED = PAIR_ROWS * PACK
 HALVES = 2
 
 
-def features_to_partitions(nc, psum, identity, rows, grouped, copy):
-    turned = psum.tile([P, HALVES, PAIR_ROWS], F32, tag="turned")
+def turn_rows(nc, turned, identity, rows):
     for h in range(HALVES):
         for t in range(PAIR):
             nc.tensor.transpose(
@@ -33,6 +33,9 @@ def features_to_partitions(nc, psum, identity, rows, grouped, copy):
                 in_=rows[:, t, :].bitcast(F32)[:, h * P : (h + 1) * P],
                 identity=identity,
             )
+
+
+def group_words(copy, grouped, turned):
     copy(
         out=grouped.bitcast(F32).rearrange("p (r h) -> p r h", h=HALVES),
         in_=turned[:].rearrange("p h r -> p r h"),
@@ -44,36 +47,147 @@ def tile_advancedkanlayer_pa_t_kernel(tc, x_norm, spline_weight, base_activation
     with ExitStack() as stack:
         consts = stack.enter_context(tc.tile_pool(name="consts", bufs=1))
         weights = stack.enter_context(tc.tile_pool(name="weights", bufs=1))
-        loads = stack.enter_context(tc.tile_pool(name="loads", bufs=4))
-        from_scalar = stack.enter_context(tc.tile_pool(name="from_scalar", bufs=3))
-        from_vector = stack.enter_context(tc.tile_pool(name="from_vector", bufs=2))
-        operands = stack.enter_context(tc.tile_pool(name="operands", bufs=3))
-        results = stack.enter_context(tc.tile_pool(name="results", bufs=3))
-        turn_psum = stack.enter_context(tc.psum_pool(name="turn_psum", bufs=2))
-        acc_psum = stack.enter_context(tc.psum_pool(name="acc_psum", bufs=3))
-
-        knots = consts.tile([P, KNOTS], BF16)
-        nc.scalar.dma_start(out=knots[:], in_=grid_points.partition_broadcast(P))
-        minus_two_knots = consts.tile([P, KNOTS], F32)
-        nc.vector.tensor_scalar_mul(out=minus_two_knots[:], in0=knots[:], scalar1=-2.0)
-        minus_one = consts.tile([P, 1], F32)
-        nc.vector.memset(minus_one[:], -1.0)
-        identity = consts.tile([P, P], F32)
-        make_identity(nc, identity[:])
+        twice = stack.enter_context(tc.tile_pool(name="twice", bufs=2))
+        thrice = stack.enter_context(tc.tile_pool(name="thrice", bufs=3))
+        psum = stack.enter_context(tc.psum_pool(name="psum", bufs=2))
+        stack.enter_context(tc.manual_schedule())
 
         x_view = x_norm.rearrange("(p t) i -> p t i", t=ROW_TILES)
         out_view = out.rearrange("(p t) o -> p t o", t=ROW_TILES)
 
-        x_rows = {}
-        x_rows[0] = loads.tile([P, PAIR, FEATURES], BF16, name="x_rows", tag="x_rows")
-        nc.sync.dma_start(out=x_rows[0][:], in_=x_view[:, 0:PAIR, :])
-        out_tiles = OUTPUTS // P
-        w_rows = weights.tile([P, out_tiles, FEATURES * KNOTS], BF16)
+        knots = consts.tile([P, KNOTS], BF16)
+        nc.scalar.dma_start(out=knots[:], in_=grid_points.partition_broadcast(P))
+        w_rows = weights.tile([P, OUT_TILES, FEATURES * KNOTS], BF16)
         nc.sync.dma_start(out=w_rows[:], in_=spline_weight.rearrange("(c p) i g -> p c (i g)", p=P))
-        a_rows = weights.tile([P, out_tiles, FEATURES], BF16)
+        x_rows = consts.tile([P, ROW_TILES, FEATURES], BF16)
+        nc.sync.dma_start(out=x_rows[:, 0:PAIR, :], in_=x_view[:, 0:PAIR, :])
+        a_rows = weights.tile([P, OUT_TILES, FEATURES], BF16)
         nc.sync.dma_start(out=a_rows[:], in_=base_activation.rearrange("(c p) i -> p c i", p=P))
+        for k in range(1, ROUNDS):
+            nc.sync.dma_start(
+                out=x_rows[:, k * PAIR : (k + 1) * PAIR, :], in_=x_view[:, k * PAIR : (k + 1) * PAIR, :]
+            )
 
-        knot_rows = weights.tile([P, KNOTS, out_tiles, FEATURES], BF16)
+        identity = consts.tile([P, P], F32)
+        make_identity(nc, identity[:])
+        minus_two_knots = consts.tile([P, KNOTS], F32)
+        nc.vector.tensor_scalar_mul(out=minus_two_knots[:], in0=knots[:], scalar1=-2.0)
+        minus_one = consts.tile([P, 1], F32)
+        nc.vector.memset(minus_one[:], -1.0)
+
+        turned_x, x_grouped, x_codes, x_scales = {}, {}, {}, {}
+        dist, outer_sq, inner_sq, outer_cube, inner_cube, signed, basis = {}, {}, {}, {}, {}, {}, {}
+        basis_codes, basis_scales, base_acc, spline_acc, tenth, result = {}, {}, {}, {}, {}, {}
+
+        def live(k):
+            return 0 <= k < ROUNDS
+
+        def turn_x(k):
+            turned_x[k] = psum.tile([P, HALVES, PAIR_ROWS], F32, name="turned_x")
+            turn_rows(nc, turned_x[k], identity[:], x_rows[:, k * PAIR : (k + 1) * PAIR, :])
+
+        def scalar_chain(k):
+            x_grouped[k] = twice.tile([P, GROUPED], BF16, align_bytes=64, name="x_grouped")
+            group_words(nc.scalar.copy, x_grouped[k][:], turned_x[k])
+            dist[k] = twice.tile([P, KNOTS, GROUPED], F32, name="dist")
+            for g in range(KNOTS):
+                nc.scalar.activation(
+                    out=dist[k][:, g, :],
+                    in_=x_grouped[k][:],
+                    func=ACT.Abs,
+                    bias=minus_two_knots[:, g : g + 1],
+                    scale=2.0,
+                )
+            outer_sq[k] = twice.tile([P, KNOTS, GROUPED], F32, name="outer_sq")
+            nc.scalar.activation(out=outer_sq[k][:], in_=dist[k][:], func=ACT.Square, bias=minus_one[:], scale=0.5)
+            inner_sq[k] = twice.tile([P, KNOTS, GROUPED], F32, name="inner_sq")
+            nc.scalar.activation(out=inner_sq[k][:], in_=dist[k][:], func=ACT.Square, bias=minus_one[:], scale=1.0)
+
+        def quantise_x(k):
+            x_codes[k] = twice.tile([P, PAIR_ROWS], U32, align_bytes=64, name="x_codes")
+            x_scales[k] = twice.tile([P, PAIR_ROWS], U8, align_bytes=64, name="x_scales")
+            nc.vector.quantize_mx(out=x_codes[k][:].bitcast(FP8X4), scales=x_scales[k][:], in_=x_grouped[k][:])
+
+        def base_product(k):
+            for t in range(PAIR):
+                base_acc[k, t] = psum.tile([P, OUTPUTS], F32, name="base_acc")
+                nc.tensor.matmul_mx(
+                    out=base_acc[k, t][:],
+                    lhsT=x_codes[k][:, t * P : (t + 1) * P].bitcast(FP8X4),
+                    lhsT_scale=x_scales[k][:, t * P : (t + 1) * P],
+                    rhs=base_codes[:].bitcast(FP8X4),
+                    rhs_scale=base_scales[:],
+                    start=True,
+                    stop=True,
+                )
+
+        def tenth_of_base(k):
+            tenth[k] = thrice.tile([P, PAIR, OUTPUTS], F32, name="tenth")
+            for t in range(PAIR):
+                nc.scalar.activation(out=tenth[k][:, t, :], in_=base_acc[k, t][:], func=ACT.Copy, scale=0.1)
+
+        def cube_outer(k):
+            outer_cube[k] = twice.tile([P, KNOTS, GROUPED], F32, name="outer_cube")
+            nc.vector.scalar_tensor_tensor(
+                out=outer_cube[k][:], in0=dist[k][:], scalar=2.0, in1=outer_sq[k][:], op0=ALU.subtract, op1=ALU.mult
+            )
+
+        def cube_inner(k):
+            inner_cube[k] = twice.tile([P, KNOTS, GROUPED], F32, name="inner_cube")
+            nc.vector.scalar_tensor_tensor(
+                out=inner_cube[k][:], in0=dist[k][:], scalar=1.0, in1=inner_sq[k][:], op0=ALU.subtract, op1=ALU.mult
+            )
+
+        def join_cubes(k):
+            signed[k] = twice.tile([P, KNOTS * GROUPED], BF16, name="signed")
+            nc.vector.scalar_tensor_tensor(
+                out=signed[k][:],
+                in0=inner_cube[k][:].rearrange("p g c -> p (g c)"),
+                scalar=0.0,
+                in1=outer_cube[k][:].rearrange("p g c -> p (g c)"),
+                op0=ALU.min,
+                op1=ALU.subtract,
+            )
+
+        def clamp(k):
+            basis[k] = twice.tile([P, KNOTS * GROUPED], BF16, align_bytes=64, name="basis")
+            nc.vector.tensor_scalar_max(out=basis[k][:], in0=signed[k][:], scalar1=0.0)
+
+        def quantise_basis(k):
+            basis_codes[k] = twice.tile([P, KNOTS * PAIR_ROWS], U32, align_bytes=64, name="basis_codes")
+            basis_scales[k] = twice.tile([P, KNOTS * PAIR_ROWS], U8, align_bytes=64, name="basis_scales")
+            nc.vector.quantize_mx(
+                out=basis_codes[k][:].bitcast(FP8X4), scales=basis_scales[k][:], in_=basis[k][:]
+            )
+
+        def spline_product(k):
+            for t in range(PAIR):
+                spline_acc[k, t] = psum.tile([P, OUTPUTS], F32, name="spline_acc")
+                for g in range(KNOTS):
+                    cols = slice(g * PAIR_ROWS + t * P, g * PAIR_ROWS + (t + 1) * P)
+                    nc.tensor.matmul_mx(
+                        out=spline_acc[k, t][:],
+                        lhsT=basis_codes[k][:, cols].bitcast(FP8X4),
+                        lhsT_scale=basis_scales[k][:, cols],
+                        rhs=knot_weights[g][0][:].bitcast(FP8X4),
+                        rhs_scale=knot_weights[g][1][:],
+                        start=(g == 0),
+                        stop=(g == KNOTS - 1),
+                    )
+
+        def add_products(k, t):
+            if t == 0:
+                result[k] = thrice.tile([P, PAIR, OUTPUTS], F32, name="result")
+            nc.vector.tensor_tensor(
+                out=result[k][:, t, :], in0=spline_acc[k, t][:], in1=tenth[k][:, t, :], op=ALU.add
+            )
+
+        def store(k):
+            nc.sync.dma_start(out=out_view[:, k * PAIR : (k + 1) * PAIR, :], in_=result[k][:])
+
+        turn_x(0)
+
+        knot_rows = weights.tile([P, KNOTS, OUT_TILES, FEATURES], BF16)
         for g in range(KNOTS):
             nc.vector.tensor_copy(
                 out=knot_rows[:, g],
@@ -81,90 +195,41 @@ def tile_advancedkanlayer_pa_t_kernel(tc, x_norm, spline_weight, base_activation
             )
 
         def quantise_weight(label, rows):
-            grouped = weights.tile([P, OUTPUTS * PACK], BF16, align_bytes=64, name="%s_grouped" % label)
-            for pair in range(out_tiles // PAIR):
-                features_to_partitions(
-                    nc,
-                    turn_psum,
-                    identity[:],
-                    rows[:, pair * PAIR : (pair + 1) * PAIR, :],
-                    grouped[:, pair * GROUPED : (pair + 1) * GROUPED],
-                    nc.vector.tensor_copy,
-                )
+            grouped = twice.tile([P, OUTPUTS * PACK], BF16, align_bytes=64, name="w_grouped")
+            for pair in range(OUT_TILES // PAIR):
+                turned_w = psum.tile([P, HALVES, PAIR_ROWS], F32, name="turned_w")
+                turn_rows(nc, turned_w, identity[:], rows[:, pair * PAIR : (pair + 1) * PAIR, :])
+                group_words(nc.vector.tensor_copy, grouped[:, pair * GROUPED : (pair + 1) * GROUPED], turned_w)
             codes = weights.tile([P, OUTPUTS], U32, align_bytes=64, name="%s_codes" % label)
             scales = weights.tile([P, OUTPUTS], U8, align_bytes=64, name="%s_scales" % label)
             nc.vector.quantize_mx(out=codes[:].bitcast(FP8X4), scales=scales[:], in_=grouped[:])
             return codes, scales
 
-        knot_weights = [quantise_weight("knot%d" % g, knot_rows[:, g]) for g in range(KNOTS)]
         base_codes, base_scales = quantise_weight("base", a_rows[:])
+        knot_weights = [quantise_weight("knot%d" % g, knot_rows[:, g]) for g in range(KNOTS)]
 
-        for r in range(ROUNDS):
-            tiles = slice(r * PAIR, (r + 1) * PAIR)
-            if r > 0:
-                x_rows[r] = loads.tile([P, PAIR, FEATURES], BF16, name="x_rows", tag="x_rows")
-                nc.sync.dma_start(out=x_rows[r][:], in_=x_view[:, tiles, :])
-
-            x_grouped = from_scalar.tile([P, GROUPED], BF16, align_bytes=64)
-            features_to_partitions(nc, turn_psum, identity[:], x_rows[r][:], x_grouped[:], nc.scalar.copy)
-            x_codes = operands.tile([P, PAIR_ROWS], U32, align_bytes=64)
-            x_scales = operands.tile([P, PAIR_ROWS], U8, align_bytes=64)
-            nc.vector.quantize_mx(out=x_codes[:].bitcast(FP8X4), scales=x_scales[:], in_=x_grouped[:])
-
-            dist = from_scalar.tile([P, KNOTS, GROUPED], F32)
-            for g in range(KNOTS):
-                nc.scalar.activation(
-                    out=dist[:, g, :], in_=x_grouped[:], func=ACT.Abs, bias=minus_two_knots[:, g : g + 1], scale=2.0
-                )
-            outer_sq = from_scalar.tile([P, KNOTS, GROUPED], F32)
-            nc.scalar.activation(out=outer_sq[:], in_=dist[:], func=ACT.Square, bias=minus_one[:], scale=0.5)
-            inner_sq = from_scalar.tile([P, KNOTS, GROUPED], F32)
-            nc.scalar.activation(out=inner_sq[:], in_=dist[:], func=ACT.Square, bias=minus_one[:], scale=1.0)
-            outer_cube = from_vector.tile([P, KNOTS, GROUPED], F32)
-            nc.vector.scalar_tensor_tensor(
-                out=outer_cube[:], in0=dist[:], scalar=2.0, in1=outer_sq[:], op0=ALU.subtract, op1=ALU.mult
-            )
-            inner_cube = from_vector.tile([P, KNOTS, GROUPED], F32)
-            nc.vector.scalar_tensor_tensor(
-                out=inner_cube[:], in0=dist[:], scalar=1.0, in1=inner_sq[:], op0=ALU.subtract, op1=ALU.mult
-            )
-            signed = from_vector.tile([P, KNOTS, GROUPED], BF16)
-            nc.vector.scalar_tensor_tensor(
-                out=signed[:], in0=inner_cube[:], scalar=0.0, in1=outer_cube[:], op0=ALU.min, op1=ALU.subtract
-            )
-            basis = from_vector.tile([P, KNOTS * GROUPED], BF16, align_bytes=64)
-            nc.vector.tensor_scalar_max(
-                out=basis[:], in0=signed[:].rearrange("p g c -> p (g c)"), scalar1=0.0
-            )
-            basis_codes = operands.tile([P, KNOTS * PAIR_ROWS], U32, align_bytes=64)
-            basis_scales = operands.tile([P, KNOTS * PAIR_ROWS], U8, align_bytes=64)
-            nc.vector.quantize_mx(out=basis_codes[:].bitcast(FP8X4), scales=basis_scales[:], in_=basis[:])
-
-            result = results.tile([P, PAIR, OUTPUTS], F32)
-            for t in range(PAIR):
-                spline_acc = acc_psum.tile([P, OUTPUTS], F32)
-                for g in range(KNOTS):
-                    cols = slice(g * PAIR_ROWS + t * P, g * PAIR_ROWS + (t + 1) * P)
-                    nc.tensor.matmul_mx(
-                        out=spline_acc[:],
-                        lhsT=basis_codes[:, cols].bitcast(FP8X4),
-                        lhsT_scale=basis_scales[:, cols],
-                        rhs=knot_weights[g][0][:].bitcast(FP8X4),
-                        rhs_scale=knot_weights[g][1][:],
-                        start=(g == 0),
-                        stop=(g == KNOTS - 1),
-                    )
-                base_acc = acc_psum.tile([P, OUTPUTS], F32)
-                nc.tensor.matmul_mx(
-                    out=base_acc[:],
-                    lhsT=x_codes[:, t * P : (t + 1) * P].bitcast(FP8X4),
-                    lhsT_scale=x_scales[:, t * P : (t + 1) * P],
-                    rhs=base_codes[:].bitcast(FP8X4),
-                    rhs_scale=base_scales[:],
-                    start=True,
-                    stop=True,
-                )
-                tenth = results.tile([P, OUTPUTS], F32)
-                nc.scalar.activation(out=tenth[:], in_=base_acc[:], func=ACT.Copy, scale=0.1)
-                nc.vector.tensor_tensor(out=result[:, t, :], in0=spline_acc[:], in1=tenth[:], op=ALU.add)
-            nc.sync.dma_start(out=out_view[:, tiles, :], in_=result[:])
+        for s in range(-1, ROUNDS + 1):
+            if live(s + 1):
+                scalar_chain(s + 1)
+            if live(s):
+                cube_outer(s)
+            if live(s - 1):
+                quantise_basis(s - 1)
+                spline_product(s - 1)
+            if live(s):
+                cube_inner(s)
+            if live(s + 1):
+                quantise_x(s + 1)
+                base_product(s + 1)
+                tenth_of_base(s + 1)
+            if live(s + 2):
+                turn_x(s + 2)
+            if live(s):
+                join_cubes(s)
+            if live(s - 1):
+                add_products(s - 1, 0)
+            if live(s):
+                clamp(s)
+            if live(s - 1):
+                add_products(s - 1, 1)
+                store(s - 1)

@@ -22,7 +22,9 @@ PAIR = 2
 PAIR_ROWS = PAIR * P
 ROUNDS = ROW_TILES // PAIR
 GROUPED = PAIR_ROWS * PACK
+UNIT = P * PACK
 HALVES = 2
+GPSIMD_KNOTS = 1
 
 
 def turn_rows(nc, turned, identity, rows):
@@ -42,14 +44,19 @@ def group_words(copy, grouped, turned):
     )
 
 
+def by_row(columns):
+    return columns.rearrange("p (r j) -> p r j", j=PACK)
+
+
 def tile_advancedkanlayer_pa_t_kernel(tc, x_norm, spline_weight, base_activation, grid_points, out):
     nc = tc.nc
     with ExitStack() as stack:
         consts = stack.enter_context(tc.tile_pool(name="consts", bufs=1))
         weights = stack.enter_context(tc.tile_pool(name="weights", bufs=1))
         twice = stack.enter_context(tc.tile_pool(name="twice", bufs=2))
-        thrice = stack.enter_context(tc.tile_pool(name="thrice", bufs=3))
-        psum = stack.enter_context(tc.psum_pool(name="psum", bufs=2))
+        ring_psum = stack.enter_context(tc.psum_pool(name="ring_psum", bufs=4))
+        pair_psum = stack.enter_context(tc.psum_pool(name="pair_psum", bufs=2))
+        lone_psum = stack.enter_context(tc.psum_pool(name="lone_psum", bufs=1))
         stack.enter_context(tc.manual_schedule())
 
         x_view = x_norm.rearrange("(p t) i -> p t i", t=ROW_TILES)
@@ -57,10 +64,10 @@ def tile_advancedkanlayer_pa_t_kernel(tc, x_norm, spline_weight, base_activation
 
         knots = consts.tile([P, KNOTS], BF16)
         nc.scalar.dma_start(out=knots[:], in_=grid_points.partition_broadcast(P))
-        w_rows = weights.tile([P, OUT_TILES, FEATURES * KNOTS], BF16)
-        nc.sync.dma_start(out=w_rows[:], in_=spline_weight.rearrange("(c p) i g -> p c (i g)", p=P))
         x_rows = consts.tile([P, ROW_TILES, FEATURES], BF16)
         nc.sync.dma_start(out=x_rows[:, 0:PAIR, :], in_=x_view[:, 0:PAIR, :])
+        w_rows = weights.tile([P, OUT_TILES, FEATURES * KNOTS], BF16)
+        nc.sync.dma_start(out=w_rows[:], in_=spline_weight.rearrange("(c p) i g -> p c (i g)", p=P))
         a_rows = weights.tile([P, OUT_TILES, FEATURES], BF16)
         nc.sync.dma_start(out=a_rows[:], in_=base_activation.rearrange("(c p) i -> p c i", p=P))
         for k in range(1, ROUNDS):
@@ -76,84 +83,114 @@ def tile_advancedkanlayer_pa_t_kernel(tc, x_norm, spline_weight, base_activation
         nc.vector.memset(minus_one[:], -1.0)
 
         turned_x, x_grouped, x_codes, x_scales = {}, {}, {}, {}
-        dist, outer_sq, inner_sq, outer_cube, inner_cube, signed, basis = {}, {}, {}, {}, {}, {}, {}
+        dist, turned_d, outer_sq, inner_sq, outer_cube, inner_cube, signed, basis = {}, {}, {}, {}, {}, {}, {}, {}
         basis_codes, basis_scales, base_acc, spline_acc, tenth, result = {}, {}, {}, {}, {}, {}
 
         def live(k):
             return 0 <= k < ROUNDS
 
-        def turn_x(k):
-            turned_x[k] = psum.tile([P, HALVES, PAIR_ROWS], F32, name="turned_x")
-            turn_rows(nc, turned_x[k], identity[:], x_rows[:, k * PAIR : (k + 1) * PAIR, :])
+        def unit_columns(u):
+            return slice(u * UNIT, (u + 1) * UNIT)
 
-        def scalar_chain(k):
-            x_grouped[k] = twice.tile([P, GROUPED], BF16, align_bytes=64, name="x_grouped")
-            group_words(nc.scalar.copy, x_grouped[k][:], turned_x[k])
-            dist[k] = twice.tile([P, KNOTS, GROUPED], F32, name="dist")
+        def distances(k):
+            if not live(k):
+                return
+            dist[k] = twice.tile([P, KNOTS, PAIR, FEATURES], F32, name="dist")
             for g in range(KNOTS):
                 nc.scalar.activation(
-                    out=dist[k][:, g, :],
-                    in_=x_grouped[k][:],
+                    out=dist[k][:, g],
+                    in_=x_rows[:, k * PAIR : (k + 1) * PAIR, :],
                     func=ACT.Abs,
                     bias=minus_two_knots[:, g : g + 1],
                     scale=2.0,
                 )
-            outer_sq[k] = twice.tile([P, KNOTS, GROUPED], F32, name="outer_sq")
-            nc.scalar.activation(out=outer_sq[k][:], in_=dist[k][:], func=ACT.Square, bias=minus_one[:], scale=0.5)
-            inner_sq[k] = twice.tile([P, KNOTS, GROUPED], F32, name="inner_sq")
-            nc.scalar.activation(out=inner_sq[k][:], in_=dist[k][:], func=ACT.Square, bias=minus_one[:], scale=1.0)
 
-        def quantise_x(k):
-            x_codes[k] = twice.tile([P, PAIR_ROWS], U32, align_bytes=64, name="x_codes")
-            x_scales[k] = twice.tile([P, PAIR_ROWS], U8, align_bytes=64, name="x_scales")
-            nc.vector.quantize_mx(out=x_codes[k][:].bitcast(FP8X4), scales=x_scales[k][:], in_=x_grouped[k][:])
+        def turn_distances(k):
+            if not live(k):
+                return
+            for g in range(KNOTS):
+                for t in range(PAIR):
+                    bank = ring_psum.tile([P, PACK, P], F32, name="turned_d")
+                    turned_d[k, g * PAIR + t] = bank
+                    planes = dist[k][:, g, t, :].rearrange("r (h p e) -> r h e p", h=HALVES, e=2)
+                    for j in range(PACK):
+                        nc.tensor.transpose(out=bank[:, j, :], in_=planes[:, j // 2, j % 2, :], identity=identity[:])
 
-        def base_product(k):
-            for t in range(PAIR):
-                base_acc[k, t] = psum.tile([P, OUTPUTS], F32, name="base_acc")
-                nc.tensor.matmul_mx(
-                    out=base_acc[k, t][:],
-                    lhsT=x_codes[k][:, t * P : (t + 1) * P].bitcast(FP8X4),
-                    lhsT_scale=x_scales[k][:, t * P : (t + 1) * P],
-                    rhs=base_codes[:].bitcast(FP8X4),
-                    rhs_scale=base_scales[:],
-                    start=True,
-                    stop=True,
+        def squares(k, u):
+            if not live(k):
+                return
+            if u == 0:
+                outer_sq[k] = twice.tile([P, KNOTS * GROUPED], F32, name="outer_sq")
+                inner_sq[k] = twice.tile([P, KNOTS * GROUPED], F32, name="inner_sq")
+            d_by_row = turned_d[k, u][:].rearrange("p j r -> p r j")
+            nc.scalar.activation(
+                out=by_row(outer_sq[k][:, unit_columns(u)]), in_=d_by_row, func=ACT.Square, bias=minus_one[:], scale=0.5
+            )
+            nc.scalar.activation(
+                out=by_row(inner_sq[k][:, unit_columns(u)]), in_=d_by_row, func=ACT.Square, bias=minus_one[:], scale=1.0
+            )
+
+        def cubes(k, u):
+            if not live(k):
+                return
+            if u == 0:
+                outer_cube[k] = twice.tile([P, KNOTS * GROUPED], F32, name="outer_cube")
+                inner_cube[k] = twice.tile([P, KNOTS * GROUPED], F32, name="inner_cube")
+            d_by_row = turned_d[k, u][:].rearrange("p j r -> p r j")
+            nc.vector.scalar_tensor_tensor(
+                out=by_row(inner_cube[k][:, unit_columns(u)]),
+                in0=d_by_row,
+                scalar=1.0,
+                in1=by_row(inner_sq[k][:, unit_columns(u)]),
+                op0=ALU.subtract,
+                op1=ALU.mult,
+            )
+            nc.vector.scalar_tensor_tensor(
+                out=by_row(outer_cube[k][:, unit_columns(u)]),
+                in0=d_by_row,
+                scalar=2.0,
+                in1=by_row(outer_sq[k][:, unit_columns(u)]),
+                op0=ALU.subtract,
+                op1=ALU.mult,
+            )
+
+        def join_cubes(k, g):
+            if not live(k):
+                return
+            if g == 0:
+                signed[k] = twice.tile([P, KNOTS * GROUPED], BF16, name="signed")
+            cols = slice(g * GROUPED, (g + 1) * GROUPED)
+            if g < GPSIMD_KNOTS:
+                nc.gpsimd.tensor_scalar(
+                    out=inner_cube[k][:, cols],
+                    in0=inner_cube[k][:, cols],
+                    scalar1=0.0,
+                    scalar2=-1.0,
+                    op0=ALU.min,
+                    op1=ALU.max,
+                )
+                nc.gpsimd.tensor_tensor(
+                    out=signed[k][:, cols], in0=inner_cube[k][:, cols], in1=outer_cube[k][:, cols], op=ALU.subtract
+                )
+            else:
+                nc.vector.scalar_tensor_tensor(
+                    out=signed[k][:, cols],
+                    in0=inner_cube[k][:, cols],
+                    scalar=0.0,
+                    in1=outer_cube[k][:, cols],
+                    op0=ALU.min,
+                    op1=ALU.subtract,
                 )
 
-        def tenth_of_base(k):
-            tenth[k] = thrice.tile([P, PAIR, OUTPUTS], F32, name="tenth")
-            for t in range(PAIR):
-                nc.scalar.activation(out=tenth[k][:, t, :], in_=base_acc[k, t][:], func=ACT.Copy, scale=0.1)
-
-        def cube_outer(k):
-            outer_cube[k] = twice.tile([P, KNOTS, GROUPED], F32, name="outer_cube")
-            nc.vector.scalar_tensor_tensor(
-                out=outer_cube[k][:], in0=dist[k][:], scalar=2.0, in1=outer_sq[k][:], op0=ALU.subtract, op1=ALU.mult
-            )
-
-        def cube_inner(k):
-            inner_cube[k] = twice.tile([P, KNOTS, GROUPED], F32, name="inner_cube")
-            nc.vector.scalar_tensor_tensor(
-                out=inner_cube[k][:], in0=dist[k][:], scalar=1.0, in1=inner_sq[k][:], op0=ALU.subtract, op1=ALU.mult
-            )
-
-        def join_cubes(k):
-            signed[k] = twice.tile([P, KNOTS * GROUPED], BF16, name="signed")
-            nc.vector.scalar_tensor_tensor(
-                out=signed[k][:],
-                in0=inner_cube[k][:].rearrange("p g c -> p (g c)"),
-                scalar=0.0,
-                in1=outer_cube[k][:].rearrange("p g c -> p (g c)"),
-                op0=ALU.min,
-                op1=ALU.subtract,
-            )
-
         def clamp(k):
+            if not live(k):
+                return
             basis[k] = twice.tile([P, KNOTS * GROUPED], BF16, align_bytes=64, name="basis")
             nc.vector.tensor_scalar_max(out=basis[k][:], in0=signed[k][:], scalar1=0.0)
 
         def quantise_basis(k):
+            if not live(k):
+                return
             basis_codes[k] = twice.tile([P, KNOTS * PAIR_ROWS], U32, align_bytes=64, name="basis_codes")
             basis_scales[k] = twice.tile([P, KNOTS * PAIR_ROWS], U8, align_bytes=64, name="basis_scales")
             nc.vector.quantize_mx(
@@ -161,8 +198,10 @@ def tile_advancedkanlayer_pa_t_kernel(tc, x_norm, spline_weight, base_activation
             )
 
         def spline_product(k):
+            if not live(k):
+                return
             for t in range(PAIR):
-                spline_acc[k, t] = psum.tile([P, OUTPUTS], F32, name="spline_acc")
+                spline_acc[k, t] = pair_psum.tile([P, OUTPUTS], F32, name="spline_acc")
                 for g in range(KNOTS):
                     cols = slice(g * PAIR_ROWS + t * P, g * PAIR_ROWS + (t + 1) * P)
                     nc.tensor.matmul_mx(
@@ -175,17 +214,64 @@ def tile_advancedkanlayer_pa_t_kernel(tc, x_norm, spline_weight, base_activation
                         stop=(g == KNOTS - 1),
                     )
 
-        def add_products(k, t):
+        def turn_x(k):
+            if not live(k):
+                return
+            turned_x[k] = lone_psum.tile([P, HALVES, PAIR_ROWS], F32, name="turned_x")
+            turn_rows(nc, turned_x[k], identity[:], x_rows[:, k * PAIR : (k + 1) * PAIR, :])
+
+        def group_x(k):
+            if not live(k):
+                return
+            x_grouped[k] = twice.tile([P, GROUPED], BF16, align_bytes=64, name="x_grouped")
+            group_words(nc.scalar.copy, x_grouped[k][:], turned_x[k])
+
+        def quantise_x(k):
+            if not live(k):
+                return
+            x_codes[k] = twice.tile([P, PAIR_ROWS], U32, align_bytes=64, name="x_codes")
+            x_scales[k] = twice.tile([P, PAIR_ROWS], U8, align_bytes=64, name="x_scales")
+            nc.vector.quantize_mx(out=x_codes[k][:].bitcast(FP8X4), scales=x_scales[k][:], in_=x_grouped[k][:])
+
+        def base_product(k, t):
+            if not live(k):
+                return
+            base_acc[k, t] = lone_psum.tile([P, OUTPUTS], F32, name="base_acc")
+            nc.tensor.matmul_mx(
+                out=base_acc[k, t][:],
+                lhsT=x_codes[k][:, t * P : (t + 1) * P].bitcast(FP8X4),
+                lhsT_scale=x_scales[k][:, t * P : (t + 1) * P],
+                rhs=base_codes[:].bitcast(FP8X4),
+                rhs_scale=base_scales[:],
+                start=True,
+                stop=True,
+            )
+
+        def tenth_of_base(k, t):
+            if not live(k):
+                return
             if t == 0:
-                result[k] = thrice.tile([P, PAIR, OUTPUTS], F32, name="result")
+                tenth[k] = twice.tile([P, PAIR, OUTPUTS], F32, name="tenth")
+            nc.scalar.activation(out=tenth[k][:, t, :], in_=base_acc[k, t][:], func=ACT.Copy, scale=0.1)
+
+        def add_products(k, t):
+            if not live(k):
+                return
+            if t == 0:
+                result[k] = twice.tile([P, PAIR, OUTPUTS], F32, name="result")
             nc.vector.tensor_tensor(
                 out=result[k][:, t, :], in0=spline_acc[k, t][:], in1=tenth[k][:, t, :], op=ALU.add
             )
 
         def store(k):
+            if not live(k):
+                return
             nc.sync.dma_start(out=out_view[:, k * PAIR : (k + 1) * PAIR, :], in_=result[k][:])
 
+        distances(0)
         turn_x(0)
+        group_x(0)
+        turn_distances(0)
 
         knot_rows = weights.tile([P, KNOTS, OUT_TILES, FEATURES], BF16)
         for g in range(KNOTS):
@@ -197,7 +283,7 @@ def tile_advancedkanlayer_pa_t_kernel(tc, x_norm, spline_weight, base_activation
         def quantise_weight(label, rows):
             grouped = twice.tile([P, OUTPUTS * PACK], BF16, align_bytes=64, name="w_grouped")
             for pair in range(OUT_TILES // PAIR):
-                turned_w = psum.tile([P, HALVES, PAIR_ROWS], F32, name="turned_w")
+                turned_w = pair_psum.tile([P, HALVES, PAIR_ROWS], F32, name="turned_w", tag="spline_acc")
                 turn_rows(nc, turned_w, identity[:], rows[:, pair * PAIR : (pair + 1) * PAIR, :])
                 group_words(nc.vector.tensor_copy, grouped[:, pair * GROUPED : (pair + 1) * GROUPED], turned_w)
             codes = weights.tile([P, OUTPUTS], U32, align_bytes=64, name="%s_codes" % label)
@@ -208,28 +294,29 @@ def tile_advancedkanlayer_pa_t_kernel(tc, x_norm, spline_weight, base_activation
         base_codes, base_scales = quantise_weight("base", a_rows[:])
         knot_weights = [quantise_weight("knot%d" % g, knot_rows[:, g]) for g in range(KNOTS)]
 
-        for s in range(-1, ROUNDS + 1):
-            if live(s + 1):
-                scalar_chain(s + 1)
-            if live(s):
-                cube_outer(s)
-            if live(s - 1):
-                quantise_basis(s - 1)
-                spline_product(s - 1)
-            if live(s):
-                cube_inner(s)
-            if live(s + 1):
-                quantise_x(s + 1)
-                base_product(s + 1)
-                tenth_of_base(s + 1)
-            if live(s + 2):
-                turn_x(s + 2)
-            if live(s):
-                join_cubes(s)
-            if live(s - 1):
-                add_products(s - 1, 0)
-            if live(s):
-                clamp(s)
-            if live(s - 1):
-                add_products(s - 1, 1)
-                store(s - 1)
+        for s in range(ROUNDS + 1):
+            squares(s, 0)
+            cubes(s, 0)
+            quantise_x(s)
+            base_product(s, 0)
+            squares(s, 1)
+            cubes(s, 1)
+            clamp(s - 1)
+            join_cubes(s, 0)
+            squares(s, 2)
+            cubes(s, 2)
+            quantise_basis(s - 1)
+            spline_product(s - 1)
+            squares(s, 3)
+            cubes(s, 3)
+            tenth_of_base(s, 0)
+            base_product(s, 1)
+            add_products(s - 1, 0)
+            join_cubes(s, 1)
+            add_products(s - 1, 1)
+            store(s - 1)
+            distances(s + 1)
+            tenth_of_base(s, 1)
+            turn_x(s + 1)
+            group_x(s + 1)
+            turn_distances(s + 1)

@@ -22,9 +22,11 @@ PAIR = 2
 PAIR_ROWS = PAIR * P
 ROUNDS = ROW_TILES // PAIR
 GROUPED = PAIR_ROWS * PACK
-UNIT = P * PACK
 HALVES = 2
-GPSIMD_KNOTS = 1
+
+LAST_FACTOR = 0.8
+SPLINE_FACTORS = (1.0, 0.25)
+BASE_FACTORS = (0.125,)
 
 
 def turn_rows(nc, turned, identity, rows):
@@ -44,19 +46,15 @@ def group_words(copy, grouped, turned):
     )
 
 
-def by_row(columns):
-    return columns.rearrange("p (r j) -> p r j", j=PACK)
-
-
 def tile_advancedkanlayer_pa_t_kernel(tc, x_norm, spline_weight, base_activation, grid_points, out):
     nc = tc.nc
     with ExitStack() as stack:
         consts = stack.enter_context(tc.tile_pool(name="consts", bufs=1))
         weights = stack.enter_context(tc.tile_pool(name="weights", bufs=1))
         twice = stack.enter_context(tc.tile_pool(name="twice", bufs=2))
-        ring_psum = stack.enter_context(tc.psum_pool(name="ring_psum", bufs=4))
-        pair_psum = stack.enter_context(tc.psum_pool(name="pair_psum", bufs=2))
-        lone_psum = stack.enter_context(tc.psum_pool(name="lone_psum", bufs=1))
+        thrice = stack.enter_context(tc.tile_pool(name="thrice", bufs=3))
+        turn_psum = stack.enter_context(tc.psum_pool(name="turn_psum", bufs=2))
+        acc_psum = stack.enter_context(tc.psum_pool(name="acc_psum", bufs=2 * PAIR))
         stack.enter_context(tc.manual_schedule())
 
         x_view = x_norm.rearrange("(p t) i -> p t i", t=ROW_TILES)
@@ -64,10 +62,10 @@ def tile_advancedkanlayer_pa_t_kernel(tc, x_norm, spline_weight, base_activation
 
         knots = consts.tile([P, KNOTS], BF16)
         nc.scalar.dma_start(out=knots[:], in_=grid_points.partition_broadcast(P))
-        x_rows = consts.tile([P, ROW_TILES, FEATURES], BF16)
-        nc.sync.dma_start(out=x_rows[:, 0:PAIR, :], in_=x_view[:, 0:PAIR, :])
         w_rows = weights.tile([P, OUT_TILES, FEATURES * KNOTS], BF16)
         nc.sync.dma_start(out=w_rows[:], in_=spline_weight.rearrange("(c p) i g -> p c (i g)", p=P))
+        x_rows = consts.tile([P, ROW_TILES, FEATURES], BF16)
+        nc.sync.dma_start(out=x_rows[:, 0:PAIR, :], in_=x_view[:, 0:PAIR, :])
         a_rows = weights.tile([P, OUT_TILES, FEATURES], BF16)
         nc.sync.dma_start(out=a_rows[:], in_=base_activation.rearrange("(c p) i -> p c i", p=P))
         for k in range(1, ROUNDS):
@@ -83,104 +81,72 @@ def tile_advancedkanlayer_pa_t_kernel(tc, x_norm, spline_weight, base_activation
         nc.vector.memset(minus_one[:], -1.0)
 
         turned_x, x_grouped, x_codes, x_scales = {}, {}, {}, {}
-        dist, turned_d, outer_sq, inner_sq, outer_cube, inner_cube, signed, basis = {}, {}, {}, {}, {}, {}, {}, {}
-        basis_codes, basis_scales, base_acc, spline_acc, tenth, result = {}, {}, {}, {}, {}, {}
+        dist, outer_sq, inner_sq, outer_cube, inner_cube, signed, basis = {}, {}, {}, {}, {}, {}, {}
+        basis_codes, basis_scales, acc = {}, {}, {}
 
         def live(k):
             return 0 <= k < ROUNDS
 
-        def unit_columns(u):
-            return slice(u * UNIT, (u + 1) * UNIT)
-
-        def distances(k):
+        def turn_x(k):
             if not live(k):
                 return
-            dist[k] = twice.tile([P, KNOTS, PAIR, FEATURES], F32, name="dist")
+            turned_x[k] = turn_psum.tile([P, HALVES, PAIR_ROWS], F32, name="turned_x")
+            turn_rows(nc, turned_x[k], identity[:], x_rows[:, k * PAIR : (k + 1) * PAIR, :])
+
+        def scalar_chain(k):
+            if not live(k):
+                return
+            x_grouped[k] = twice.tile([P, GROUPED], BF16, align_bytes=64, name="x_grouped")
+            group_words(nc.scalar.copy, x_grouped[k][:], turned_x[k])
+            dist[k] = twice.tile([P, KNOTS, GROUPED], F32, name="dist")
             for g in range(KNOTS):
                 nc.scalar.activation(
-                    out=dist[k][:, g],
-                    in_=x_rows[:, k * PAIR : (k + 1) * PAIR, :],
+                    out=dist[k][:, g, :],
+                    in_=x_grouped[k][:],
                     func=ACT.Abs,
                     bias=minus_two_knots[:, g : g + 1],
                     scale=2.0,
                 )
+            outer_sq[k] = twice.tile([P, KNOTS, GROUPED], F32, name="outer_sq")
+            nc.scalar.activation(out=outer_sq[k][:], in_=dist[k][:], func=ACT.Square, bias=minus_one[:], scale=0.5)
+            inner_sq[k] = twice.tile([P, KNOTS, GROUPED], F32, name="inner_sq")
+            nc.scalar.activation(out=inner_sq[k][:], in_=dist[k][:], func=ACT.Square, bias=minus_one[:], scale=1.0)
 
-        def turn_distances(k):
+        def quantise_x(k):
             if not live(k):
                 return
-            for g in range(KNOTS):
-                for t in range(PAIR):
-                    bank = ring_psum.tile([P, PACK, P], F32, name="turned_d")
-                    turned_d[k, g * PAIR + t] = bank
-                    planes = dist[k][:, g, t, :].rearrange("r (h p e) -> r h e p", h=HALVES, e=2)
-                    for j in range(PACK):
-                        nc.tensor.transpose(out=bank[:, j, :], in_=planes[:, j // 2, j % 2, :], identity=identity[:])
+            x_codes[k] = thrice.tile([P, PAIR_ROWS], U32, align_bytes=64, name="x_codes")
+            x_scales[k] = thrice.tile([P, PAIR_ROWS], U8, align_bytes=64, name="x_scales")
+            nc.vector.quantize_mx(out=x_codes[k][:].bitcast(FP8X4), scales=x_scales[k][:], in_=x_grouped[k][:])
 
-        def squares(k, u):
+        def cube_outer(k):
             if not live(k):
                 return
-            if u == 0:
-                outer_sq[k] = twice.tile([P, KNOTS * GROUPED], F32, name="outer_sq")
-                inner_sq[k] = twice.tile([P, KNOTS * GROUPED], F32, name="inner_sq")
-            d_by_row = turned_d[k, u][:].rearrange("p j r -> p r j")
-            nc.scalar.activation(
-                out=by_row(outer_sq[k][:, unit_columns(u)]), in_=d_by_row, func=ACT.Square, bias=minus_one[:], scale=0.5
-            )
-            nc.scalar.activation(
-                out=by_row(inner_sq[k][:, unit_columns(u)]), in_=d_by_row, func=ACT.Square, bias=minus_one[:], scale=1.0
-            )
-
-        def cubes(k, u):
-            if not live(k):
-                return
-            if u == 0:
-                outer_cube[k] = twice.tile([P, KNOTS * GROUPED], F32, name="outer_cube")
-                inner_cube[k] = twice.tile([P, KNOTS * GROUPED], F32, name="inner_cube")
-            d_by_row = turned_d[k, u][:].rearrange("p j r -> p r j")
+            outer_cube[k] = twice.tile([P, KNOTS, GROUPED], F32, name="outer_cube")
             nc.vector.scalar_tensor_tensor(
-                out=by_row(inner_cube[k][:, unit_columns(u)]),
-                in0=d_by_row,
-                scalar=1.0,
-                in1=by_row(inner_sq[k][:, unit_columns(u)]),
-                op0=ALU.subtract,
-                op1=ALU.mult,
-            )
-            nc.vector.scalar_tensor_tensor(
-                out=by_row(outer_cube[k][:, unit_columns(u)]),
-                in0=d_by_row,
-                scalar=2.0,
-                in1=by_row(outer_sq[k][:, unit_columns(u)]),
-                op0=ALU.subtract,
-                op1=ALU.mult,
+                out=outer_cube[k][:], in0=dist[k][:], scalar=2.0, in1=outer_sq[k][:], op0=ALU.subtract, op1=ALU.mult
             )
 
-        def join_cubes(k, g):
+        def cube_inner(k):
             if not live(k):
                 return
-            if g == 0:
-                signed[k] = twice.tile([P, KNOTS * GROUPED], BF16, name="signed")
-            cols = slice(g * GROUPED, (g + 1) * GROUPED)
-            if g < GPSIMD_KNOTS:
-                nc.gpsimd.tensor_scalar(
-                    out=inner_cube[k][:, cols],
-                    in0=inner_cube[k][:, cols],
-                    scalar1=0.0,
-                    scalar2=-1.0,
-                    op0=ALU.min,
-                    op1=ALU.max,
-                )
-                nc.gpsimd.tensor_tensor(
-                    out=signed[k][:, cols], in0=inner_cube[k][:, cols], in1=outer_cube[k][:, cols], op=ALU.subtract
-                )
-            else:
-                nc.vector.scalar_tensor_tensor(
-                    out=signed[k][:, cols],
-                    in0=inner_cube[k][:, cols],
-                    scalar=0.0,
-                    in1=outer_cube[k][:, cols],
-                    op0=ALU.min,
-                    op1=ALU.subtract,
-                )
+            inner_cube[k] = twice.tile([P, KNOTS, GROUPED], F32, name="inner_cube")
+            nc.vector.scalar_tensor_tensor(
+                out=inner_cube[k][:], in0=dist[k][:], scalar=1.0, in1=inner_sq[k][:], op0=ALU.subtract, op1=ALU.mult
+            )
+
+        def join_cubes(k):
+            if not live(k):
+                return
+            signed[k] = twice.tile([P, KNOTS * GROUPED], BF16, name="signed")
+            nc.vector.scalar_tensor_tensor(
+                out=signed[k][:],
+                in0=inner_cube[k][:].rearrange("p g c -> p (g c)"),
+                scalar=0.0,
+                in1=outer_cube[k][:].rearrange("p g c -> p (g c)"),
+                op0=ALU.min,
+                op1=ALU.subtract,
+            )
 
         def clamp(k):
             if not live(k):
@@ -197,81 +163,39 @@ def tile_advancedkanlayer_pa_t_kernel(tc, x_norm, spline_weight, base_activation
                 out=basis_codes[k][:].bitcast(FP8X4), scales=basis_scales[k][:], in_=basis[k][:]
             )
 
-        def spline_product(k):
+        def products(k):
             if not live(k):
                 return
             for t in range(PAIR):
-                spline_acc[k, t] = pair_psum.tile([P, OUTPUTS], F32, name="spline_acc")
+                passes = []
                 for g in range(KNOTS):
                     cols = slice(g * PAIR_ROWS + t * P, g * PAIR_ROWS + (t + 1) * P)
+                    for moving in knot_weights[g]:
+                        passes.append((basis_codes[k][:, cols], basis_scales[k][:, cols], moving))
+                for moving in base_weights:
+                    cols = slice(t * P, (t + 1) * P)
+                    passes.append((x_codes[k][:, cols], x_scales[k][:, cols], moving))
+                acc[k, t] = acc_psum.tile([P, OUTPUTS], F32, name="acc")
+                for n, (codes, scales, moving) in enumerate(passes):
                     nc.tensor.matmul_mx(
-                        out=spline_acc[k, t][:],
-                        lhsT=basis_codes[k][:, cols].bitcast(FP8X4),
-                        lhsT_scale=basis_scales[k][:, cols],
-                        rhs=knot_weights[g][0][:].bitcast(FP8X4),
-                        rhs_scale=knot_weights[g][1][:],
-                        start=(g == 0),
-                        stop=(g == KNOTS - 1),
+                        out=acc[k, t][:],
+                        lhsT=codes.bitcast(FP8X4),
+                        lhsT_scale=scales,
+                        rhs=moving[0][:].bitcast(FP8X4),
+                        rhs_scale=moving[1][:],
+                        start=(n == 0),
+                        stop=(n == len(passes) - 1),
                     )
 
-        def turn_x(k):
+        def finish(k):
             if not live(k):
                 return
-            turned_x[k] = lone_psum.tile([P, HALVES, PAIR_ROWS], F32, name="turned_x")
-            turn_rows(nc, turned_x[k], identity[:], x_rows[:, k * PAIR : (k + 1) * PAIR, :])
+            result = thrice.tile([P, PAIR, OUTPUTS], F32, name="result")
+            for t in range(PAIR):
+                nc.scalar.activation(out=result[:, t, :], in_=acc[k, t][:], func=ACT.Copy, scale=LAST_FACTOR)
+            nc.sync.dma_start(out=out_view[:, k * PAIR : (k + 1) * PAIR, :], in_=result[:])
 
-        def group_x(k):
-            if not live(k):
-                return
-            x_grouped[k] = twice.tile([P, GROUPED], BF16, align_bytes=64, name="x_grouped")
-            group_words(nc.scalar.copy, x_grouped[k][:], turned_x[k])
-
-        def quantise_x(k):
-            if not live(k):
-                return
-            x_codes[k] = twice.tile([P, PAIR_ROWS], U32, align_bytes=64, name="x_codes")
-            x_scales[k] = twice.tile([P, PAIR_ROWS], U8, align_bytes=64, name="x_scales")
-            nc.vector.quantize_mx(out=x_codes[k][:].bitcast(FP8X4), scales=x_scales[k][:], in_=x_grouped[k][:])
-
-        def base_product(k, t):
-            if not live(k):
-                return
-            base_acc[k, t] = lone_psum.tile([P, OUTPUTS], F32, name="base_acc")
-            nc.tensor.matmul_mx(
-                out=base_acc[k, t][:],
-                lhsT=x_codes[k][:, t * P : (t + 1) * P].bitcast(FP8X4),
-                lhsT_scale=x_scales[k][:, t * P : (t + 1) * P],
-                rhs=base_codes[:].bitcast(FP8X4),
-                rhs_scale=base_scales[:],
-                start=True,
-                stop=True,
-            )
-
-        def tenth_of_base(k, t):
-            if not live(k):
-                return
-            if t == 0:
-                tenth[k] = twice.tile([P, PAIR, OUTPUTS], F32, name="tenth")
-            nc.scalar.activation(out=tenth[k][:, t, :], in_=base_acc[k, t][:], func=ACT.Copy, scale=0.1)
-
-        def add_products(k, t):
-            if not live(k):
-                return
-            if t == 0:
-                result[k] = twice.tile([P, PAIR, OUTPUTS], F32, name="result")
-            nc.vector.tensor_tensor(
-                out=result[k][:, t, :], in0=spline_acc[k, t][:], in1=tenth[k][:, t, :], op=ALU.add
-            )
-
-        def store(k):
-            if not live(k):
-                return
-            nc.sync.dma_start(out=out_view[:, k * PAIR : (k + 1) * PAIR, :], in_=result[k][:])
-
-        distances(0)
         turn_x(0)
-        group_x(0)
-        turn_distances(0)
 
         knot_rows = weights.tile([P, KNOTS, OUT_TILES, FEATURES], BF16)
         for g in range(KNOTS):
@@ -280,43 +204,35 @@ def tile_advancedkanlayer_pa_t_kernel(tc, x_norm, spline_weight, base_activation
                 in_=w_rows[:].rearrange("p c (i g) -> p g c i", g=KNOTS)[:, g],
             )
 
-        def quantise_weight(label, rows):
+        def quantise_weight(label, rows, factors):
             grouped = twice.tile([P, OUTPUTS * PACK], BF16, align_bytes=64, name="w_grouped")
             for pair in range(OUT_TILES // PAIR):
-                turned_w = pair_psum.tile([P, HALVES, PAIR_ROWS], F32, name="turned_w", tag="spline_acc")
+                turned_w = turn_psum.tile([P, HALVES, PAIR_ROWS], F32, name="turned_w")
                 turn_rows(nc, turned_w, identity[:], rows[:, pair * PAIR : (pair + 1) * PAIR, :])
                 group_words(nc.vector.tensor_copy, grouped[:, pair * GROUPED : (pair + 1) * GROUPED], turned_w)
-            codes = weights.tile([P, OUTPUTS], U32, align_bytes=64, name="%s_codes" % label)
-            scales = weights.tile([P, OUTPUTS], U8, align_bytes=64, name="%s_scales" % label)
-            nc.vector.quantize_mx(out=codes[:].bitcast(FP8X4), scales=scales[:], in_=grouped[:])
-            return codes, scales
+            operands = []
+            for n, factor in enumerate(factors):
+                scaled = grouped
+                if factor != 1.0:
+                    scaled = twice.tile([P, OUTPUTS * PACK], BF16, align_bytes=64, name="w_scaled")
+                    nc.vector.tensor_scalar_mul(out=scaled[:], in0=grouped[:], scalar1=factor)
+                codes = weights.tile([P, OUTPUTS], U32, align_bytes=64, name="%s_codes%d" % (label, n))
+                scales = weights.tile([P, OUTPUTS], U8, align_bytes=64, name="%s_scales%d" % (label, n))
+                nc.vector.quantize_mx(out=codes[:].bitcast(FP8X4), scales=scales[:], in_=scaled[:])
+                operands.append((codes, scales))
+            return operands
 
-        base_codes, base_scales = quantise_weight("base", a_rows[:])
-        knot_weights = [quantise_weight("knot%d" % g, knot_rows[:, g]) for g in range(KNOTS)]
+        base_weights = quantise_weight("base", a_rows[:], BASE_FACTORS)
+        knot_weights = [quantise_weight("knot%d" % g, knot_rows[:, g], SPLINE_FACTORS) for g in range(KNOTS)]
 
-        for s in range(ROUNDS + 1):
-            squares(s, 0)
-            cubes(s, 0)
-            quantise_x(s)
-            base_product(s, 0)
-            squares(s, 1)
-            cubes(s, 1)
+        for s in range(-1, ROUNDS + 2):
+            turn_x(s + 2)
+            scalar_chain(s + 1)
+            finish(s - 2)
+            cube_outer(s)
             clamp(s - 1)
-            join_cubes(s, 0)
-            squares(s, 2)
-            cubes(s, 2)
+            cube_inner(s)
             quantise_basis(s - 1)
-            spline_product(s - 1)
-            squares(s, 3)
-            cubes(s, 3)
-            tenth_of_base(s, 0)
-            base_product(s, 1)
-            add_products(s - 1, 0)
-            join_cubes(s, 1)
-            add_products(s - 1, 1)
-            store(s - 1)
-            distances(s + 1)
-            tenth_of_base(s, 1)
-            turn_x(s + 1)
-            group_x(s + 1)
-            turn_distances(s + 1)
+            products(s - 1)
+            join_cubes(s)
+            quantise_x(s + 1)

@@ -19,9 +19,9 @@ FLOPS = 2 * BATCH * OUTPUTS * (FEATURES * KNOTS + FEATURES)
 ROW_TILES = BATCH // P
 OUT_TILES = OUTPUTS // P
 PAIR = 2
-PAIR_ROWS = PAIR * P
-ROUNDS = ROW_TILES // PAIR
-GROUPED = PAIR_ROWS * PACK
+ROUND_TILES = [PAIR] * (ROW_TILES // PAIR - 1) + [1] * PAIR
+ROUNDS = len(ROUND_TILES)
+TILE_GROUPED = P * PACK
 HALVES = 2
 
 LAST_FACTOR = 0.8
@@ -29,9 +29,9 @@ SPLINE_FACTORS = (1.0, 0.25)
 BASE_FACTORS = (0.125,)
 
 
-def turn_rows(nc, turned, identity, rows):
+def turn_rows(nc, turned, identity, rows, tiles):
     for h in range(HALVES):
-        for t in range(PAIR):
+        for t in range(tiles):
             nc.tensor.transpose(
                 out=turned[:, h, t * P : (t + 1) * P],
                 in_=rows[:, t, :].bitcast(F32)[:, h * P : (h + 1) * P],
@@ -57,6 +57,10 @@ def tile_advancedkanlayer_pa_t_kernel(tc, x_norm, spline_weight, base_activation
         acc_psum = stack.enter_context(tc.psum_pool(name="acc_psum", bufs=2 * PAIR))
         stack.enter_context(tc.manual_schedule())
 
+        def tiles_of(k):
+            first = sum(ROUND_TILES[:k])
+            return slice(first, first + ROUND_TILES[k])
+
         x_view = x_norm.rearrange("(p t) i -> p t i", t=ROW_TILES)
         out_view = out.rearrange("(p t) o -> p t o", t=ROW_TILES)
 
@@ -65,13 +69,11 @@ def tile_advancedkanlayer_pa_t_kernel(tc, x_norm, spline_weight, base_activation
         w_rows = weights.tile([P, OUT_TILES, FEATURES * KNOTS], BF16)
         nc.sync.dma_start(out=w_rows[:], in_=spline_weight.rearrange("(c p) i g -> p c (i g)", p=P))
         x_rows = consts.tile([P, ROW_TILES, FEATURES], BF16)
-        nc.sync.dma_start(out=x_rows[:, 0:PAIR, :], in_=x_view[:, 0:PAIR, :])
+        nc.sync.dma_start(out=x_rows[:, tiles_of(0), :], in_=x_view[:, tiles_of(0), :])
         a_rows = weights.tile([P, OUT_TILES, FEATURES], BF16)
         nc.sync.dma_start(out=a_rows[:], in_=base_activation.rearrange("(c p) i -> p c i", p=P))
         for k in range(1, ROUNDS):
-            nc.sync.dma_start(
-                out=x_rows[:, k * PAIR : (k + 1) * PAIR, :], in_=x_view[:, k * PAIR : (k + 1) * PAIR, :]
-            )
+            nc.sync.dma_start(out=x_rows[:, tiles_of(k), :], in_=x_view[:, tiles_of(k), :])
 
         identity = consts.tile([P, P], F32)
         make_identity(nc, identity[:])
@@ -90,15 +92,16 @@ def tile_advancedkanlayer_pa_t_kernel(tc, x_norm, spline_weight, base_activation
         def turn_x(k):
             if not live(k):
                 return
-            turned_x[k] = turn_psum.tile([P, HALVES, PAIR_ROWS], F32, name="turned_x")
-            turn_rows(nc, turned_x[k], identity[:], x_rows[:, k * PAIR : (k + 1) * PAIR, :])
+            turned_x[k] = turn_psum.tile([P, HALVES, ROUND_TILES[k] * P], F32, name="turned_x")
+            turn_rows(nc, turned_x[k], identity[:], x_rows[:, tiles_of(k), :], ROUND_TILES[k])
 
         def scalar_chain(k):
             if not live(k):
                 return
-            x_grouped[k] = twice.tile([P, GROUPED], BF16, align_bytes=64, name="x_grouped")
+            grouped = ROUND_TILES[k] * TILE_GROUPED
+            x_grouped[k] = twice.tile([P, grouped], BF16, align_bytes=64, name="x_grouped")
             group_words(nc.scalar.copy, x_grouped[k][:], turned_x[k])
-            dist[k] = twice.tile([P, KNOTS, GROUPED], F32, name="dist")
+            dist[k] = twice.tile([P, KNOTS, grouped], F32, name="dist")
             for g in range(KNOTS):
                 nc.scalar.activation(
                     out=dist[k][:, g, :],
@@ -107,22 +110,22 @@ def tile_advancedkanlayer_pa_t_kernel(tc, x_norm, spline_weight, base_activation
                     bias=minus_two_knots[:, g : g + 1],
                     scale=2.0,
                 )
-            outer_sq[k] = twice.tile([P, KNOTS, GROUPED], F32, name="outer_sq")
+            outer_sq[k] = twice.tile([P, KNOTS, grouped], F32, name="outer_sq")
             nc.scalar.activation(out=outer_sq[k][:], in_=dist[k][:], func=ACT.Square, bias=minus_one[:], scale=0.5)
-            inner_sq[k] = twice.tile([P, KNOTS, GROUPED], F32, name="inner_sq")
+            inner_sq[k] = twice.tile([P, KNOTS, grouped], F32, name="inner_sq")
             nc.scalar.activation(out=inner_sq[k][:], in_=dist[k][:], func=ACT.Square, bias=minus_one[:], scale=1.0)
 
         def quantise_x(k):
             if not live(k):
                 return
-            x_codes[k] = thrice.tile([P, PAIR_ROWS], U32, align_bytes=64, name="x_codes")
-            x_scales[k] = thrice.tile([P, PAIR_ROWS], U8, align_bytes=64, name="x_scales")
+            x_codes[k] = thrice.tile([P, ROUND_TILES[k] * P], U32, align_bytes=64, name="x_codes")
+            x_scales[k] = thrice.tile([P, ROUND_TILES[k] * P], U8, align_bytes=64, name="x_scales")
             nc.vector.quantize_mx(out=x_codes[k][:].bitcast(FP8X4), scales=x_scales[k][:], in_=x_grouped[k][:])
 
         def cube_outer(k):
             if not live(k):
                 return
-            outer_cube[k] = twice.tile([P, KNOTS, GROUPED], F32, name="outer_cube")
+            outer_cube[k] = twice.tile([P, KNOTS, ROUND_TILES[k] * TILE_GROUPED], F32, name="outer_cube")
             nc.vector.scalar_tensor_tensor(
                 out=outer_cube[k][:], in0=dist[k][:], scalar=2.0, in1=outer_sq[k][:], op0=ALU.subtract, op1=ALU.mult
             )
@@ -130,7 +133,7 @@ def tile_advancedkanlayer_pa_t_kernel(tc, x_norm, spline_weight, base_activation
         def cube_inner(k):
             if not live(k):
                 return
-            inner_cube[k] = twice.tile([P, KNOTS, GROUPED], F32, name="inner_cube")
+            inner_cube[k] = twice.tile([P, KNOTS, ROUND_TILES[k] * TILE_GROUPED], F32, name="inner_cube")
             nc.vector.scalar_tensor_tensor(
                 out=inner_cube[k][:], in0=dist[k][:], scalar=1.0, in1=inner_sq[k][:], op0=ALU.subtract, op1=ALU.mult
             )
@@ -138,7 +141,7 @@ def tile_advancedkanlayer_pa_t_kernel(tc, x_norm, spline_weight, base_activation
         def join_cubes(k):
             if not live(k):
                 return
-            signed[k] = twice.tile([P, KNOTS * GROUPED], BF16, name="signed")
+            signed[k] = twice.tile([P, KNOTS * ROUND_TILES[k] * TILE_GROUPED], BF16, name="signed")
             nc.vector.scalar_tensor_tensor(
                 out=signed[k][:],
                 in0=inner_cube[k][:].rearrange("p g c -> p (g c)"),
@@ -151,14 +154,14 @@ def tile_advancedkanlayer_pa_t_kernel(tc, x_norm, spline_weight, base_activation
         def clamp(k):
             if not live(k):
                 return
-            basis[k] = twice.tile([P, KNOTS * GROUPED], BF16, align_bytes=64, name="basis")
+            basis[k] = twice.tile([P, KNOTS * ROUND_TILES[k] * TILE_GROUPED], BF16, align_bytes=64, name="basis")
             nc.vector.tensor_scalar_max(out=basis[k][:], in0=signed[k][:], scalar1=0.0)
 
         def quantise_basis(k):
             if not live(k):
                 return
-            basis_codes[k] = twice.tile([P, KNOTS * PAIR_ROWS], U32, align_bytes=64, name="basis_codes")
-            basis_scales[k] = twice.tile([P, KNOTS * PAIR_ROWS], U8, align_bytes=64, name="basis_scales")
+            basis_codes[k] = twice.tile([P, KNOTS * ROUND_TILES[k] * P], U32, align_bytes=64, name="basis_codes")
+            basis_scales[k] = twice.tile([P, KNOTS * ROUND_TILES[k] * P], U8, align_bytes=64, name="basis_scales")
             nc.vector.quantize_mx(
                 out=basis_codes[k][:].bitcast(FP8X4), scales=basis_scales[k][:], in_=basis[k][:]
             )
@@ -166,10 +169,11 @@ def tile_advancedkanlayer_pa_t_kernel(tc, x_norm, spline_weight, base_activation
         def products(k):
             if not live(k):
                 return
-            for t in range(PAIR):
+            for t in range(ROUND_TILES[k]):
                 passes = []
                 for g in range(KNOTS):
-                    cols = slice(g * PAIR_ROWS + t * P, g * PAIR_ROWS + (t + 1) * P)
+                    first = (g * ROUND_TILES[k] + t) * P
+                    cols = slice(first, first + P)
                     for moving in knot_weights[g]:
                         passes.append((basis_codes[k][:, cols], basis_scales[k][:, cols], moving))
                 for moving in base_weights:
@@ -190,10 +194,10 @@ def tile_advancedkanlayer_pa_t_kernel(tc, x_norm, spline_weight, base_activation
         def finish(k):
             if not live(k):
                 return
-            result = thrice.tile([P, PAIR, OUTPUTS], F32, name="result")
-            for t in range(PAIR):
+            result = thrice.tile([P, ROUND_TILES[k], OUTPUTS], F32, name="result")
+            for t in range(ROUND_TILES[k]):
                 nc.scalar.activation(out=result[:, t, :], in_=acc[k, t][:], func=ACT.Copy, scale=LAST_FACTOR)
-            nc.sync.dma_start(out=out_view[:, k * PAIR : (k + 1) * PAIR, :], in_=result[:])
+            nc.sync.dma_start(out=out_view[:, tiles_of(k), :], in_=result[:])
 
         turn_x(0)
 
@@ -207,9 +211,10 @@ def tile_advancedkanlayer_pa_t_kernel(tc, x_norm, spline_weight, base_activation
         def quantise_weight(label, rows, factors):
             grouped = twice.tile([P, OUTPUTS * PACK], BF16, align_bytes=64, name="w_grouped")
             for pair in range(OUT_TILES // PAIR):
-                turned_w = turn_psum.tile([P, HALVES, PAIR_ROWS], F32, name="turned_w")
-                turn_rows(nc, turned_w, identity[:], rows[:, pair * PAIR : (pair + 1) * PAIR, :])
-                group_words(nc.vector.tensor_copy, grouped[:, pair * GROUPED : (pair + 1) * GROUPED], turned_w)
+                turned_w = turn_psum.tile([P, HALVES, PAIR * P], F32, name="turned_w")
+                turn_rows(nc, turned_w, identity[:], rows[:, pair * PAIR : (pair + 1) * PAIR, :], PAIR)
+                columns = slice(pair * PAIR * TILE_GROUPED, (pair + 1) * PAIR * TILE_GROUPED)
+                group_words(nc.vector.tensor_copy, grouped[:, columns], turned_w)
             operands = []
             for n, factor in enumerate(factors):
                 scaled = grouped

@@ -19,7 +19,7 @@ FLOPS = 2 * BATCH * OUTPUTS * (FEATURES * KNOTS + FEATURES)
 ROW_TILES = BATCH // P
 OUT_TILES = OUTPUTS // P
 PAIR = 2
-ROUND_TILES = [PAIR] * (ROW_TILES // PAIR - 1) + [1] * PAIR
+ROUND_TILES = [1] * PAIR + [PAIR] * (ROW_TILES // PAIR - 2) + [1] * PAIR
 ROUNDS = len(ROUND_TILES)
 TILE_GROUPED = P * PACK
 HALVES = 2
@@ -66,13 +66,14 @@ def tile_advancedkanlayer_pa_t_kernel(tc, x_norm, spline_weight, base_activation
 
         knots = consts.tile([P, KNOTS], BF16)
         nc.scalar.dma_start(out=knots[:], in_=grid_points.partition_broadcast(P))
-        w_rows = weights.tile([P, OUT_TILES, FEATURES * KNOTS], BF16)
-        nc.sync.dma_start(out=w_rows[:], in_=spline_weight.rearrange("(c p) i g -> p c (i g)", p=P))
         x_rows = consts.tile([P, ROW_TILES, FEATURES], BF16)
-        nc.sync.dma_start(out=x_rows[:, tiles_of(0), :], in_=x_view[:, tiles_of(0), :])
+        for k in range(2):
+            nc.sync.dma_start(out=x_rows[:, tiles_of(k), :], in_=x_view[:, tiles_of(k), :])
         a_rows = weights.tile([P, OUT_TILES, FEATURES], BF16)
         nc.sync.dma_start(out=a_rows[:], in_=base_activation.rearrange("(c p) i -> p c i", p=P))
-        for k in range(1, ROUNDS):
+        w_rows = weights.tile([P, OUT_TILES, FEATURES * KNOTS], BF16)
+        nc.sync.dma_start(out=w_rows[:], in_=spline_weight.rearrange("(c p) i g -> p c (i g)", p=P))
+        for k in range(2, ROUNDS):
             nc.sync.dma_start(out=x_rows[:, tiles_of(k), :], in_=x_view[:, tiles_of(k), :])
 
         identity = consts.tile([P, P], F32)
@@ -105,7 +106,7 @@ def tile_advancedkanlayer_pa_t_kernel(tc, x_norm, spline_weight, base_activation
             for g in range(KNOTS):
                 nc.scalar.activation(
                     out=dist[k][:, g, :],
-                    in_=x_grouped[k][:],
+                    in_=turned_x[k][:].rearrange("p h r -> p (h r)").bitcast(BF16),
                     func=ACT.Abs,
                     bias=minus_two_knots[:, g : g + 1],
                     scale=2.0,
@@ -143,10 +144,10 @@ def tile_advancedkanlayer_pa_t_kernel(tc, x_norm, spline_weight, base_activation
                 return
             signed[k] = twice.tile([P, KNOTS * ROUND_TILES[k] * TILE_GROUPED], BF16, name="signed")
             nc.vector.scalar_tensor_tensor(
-                out=signed[k][:],
-                in0=inner_cube[k][:].rearrange("p g c -> p (g c)"),
+                out=signed[k][:].rearrange("p (c g) -> p c g", g=KNOTS),
+                in0=inner_cube[k][:].rearrange("p g c -> p c g"),
                 scalar=0.0,
-                in1=outer_cube[k][:].rearrange("p g c -> p (g c)"),
+                in1=outer_cube[k][:].rearrange("p g c -> p c g"),
                 op0=ALU.min,
                 op1=ALU.subtract,
             )
@@ -171,14 +172,14 @@ def tile_advancedkanlayer_pa_t_kernel(tc, x_norm, spline_weight, base_activation
                 return
             for t in range(ROUND_TILES[k]):
                 passes = []
-                for g in range(KNOTS):
-                    first = (g * ROUND_TILES[k] + t) * P
-                    cols = slice(first, first + P)
-                    for moving in knot_weights[g]:
-                        passes.append((basis_codes[k][:, cols], basis_scales[k][:, cols], moving))
                 for moving in base_weights:
                     cols = slice(t * P, (t + 1) * P)
                     passes.append((x_codes[k][:, cols], x_scales[k][:, cols], moving))
+                for h in range(HALVES):
+                    first = (h * ROUND_TILES[k] + t) * P
+                    cols = slice(first, first + P)
+                    for moving in spline_weights[h]:
+                        passes.append((basis_codes[k][:, cols], basis_scales[k][:, cols], moving))
                 acc[k, t] = acc_psum.tile([P, OUTPUTS], F32, name="acc")
                 for n, (codes, scales, moving) in enumerate(passes):
                     nc.tensor.matmul_mx(
@@ -199,22 +200,31 @@ def tile_advancedkanlayer_pa_t_kernel(tc, x_norm, spline_weight, base_activation
                 nc.scalar.activation(out=result[:, t, :], in_=acc[k, t][:], func=ACT.Copy, scale=LAST_FACTOR)
             nc.sync.dma_start(out=out_view[:, tiles_of(k), :], in_=result[:])
 
-        turn_x(0)
+        def turn_base(turned, c, t):
+            turn_rows(nc, turned[:, :, t * P : (t + 1) * P], identity[:], a_rows[:, c : c + 1, :], 1)
 
-        knot_rows = weights.tile([P, KNOTS, OUT_TILES, FEATURES], BF16)
-        for g in range(KNOTS):
-            nc.vector.tensor_copy(
-                out=knot_rows[:, g],
-                in_=w_rows[:].rearrange("p c (i g) -> p g c i", g=KNOTS)[:, g],
-            )
+        def turn_spline(h):
+            def turn(turned, c, t):
+                for e in range(2):
+                    nc.tensor.transpose(
+                        out=turned[:, e, t * P : (t + 1) * P],
+                        in_=w_rows[:, c, :].bitcast(F32)[:, 2 * P * h + e : 2 * P * (h + 1) : 2],
+                        identity=identity[:],
+                    )
 
-        def quantise_weight(label, rows, factors):
+            return turn
+
+        def group_weight(copy, turn):
             grouped = twice.tile([P, OUTPUTS * PACK], BF16, align_bytes=64, name="w_grouped")
             for pair in range(OUT_TILES // PAIR):
                 turned_w = turn_psum.tile([P, HALVES, PAIR * P], F32, name="turned_w")
-                turn_rows(nc, turned_w, identity[:], rows[:, pair * PAIR : (pair + 1) * PAIR, :], PAIR)
+                for t in range(PAIR):
+                    turn(turned_w, pair * PAIR + t, t)
                 columns = slice(pair * PAIR * TILE_GROUPED, (pair + 1) * PAIR * TILE_GROUPED)
-                group_words(nc.vector.tensor_copy, grouped[:, columns], turned_w)
+                group_words(copy, grouped[:, columns], turned_w)
+            return grouped
+
+        def quantise_weight(label, grouped, factors):
             operands = []
             for n, factor in enumerate(factors):
                 scaled = grouped
@@ -227,17 +237,27 @@ def tile_advancedkanlayer_pa_t_kernel(tc, x_norm, spline_weight, base_activation
                 operands.append((codes, scales))
             return operands
 
-        base_weights = quantise_weight("base", a_rows[:], BASE_FACTORS)
-        knot_weights = [quantise_weight("knot%d" % g, knot_rows[:, g], SPLINE_FACTORS) for g in range(KNOTS)]
+        spline_weights, spline_grouped = {}, {}
 
-        for s in range(-1, ROUNDS + 2):
+        turn_x(0)
+        scalar_chain(0)
+        turn_x(1)
+        base_grouped = group_weight(nc.vector.tensor_copy, turn_base)
+        base_weights = quantise_weight("base", base_grouped, BASE_FACTORS)
+        quantise_x(0)
+
+        for s in range(ROUNDS + 2):
             turn_x(s + 2)
             scalar_chain(s + 1)
+            if s < HALVES:
+                spline_grouped[s] = group_weight(nc.scalar.copy, turn_spline(s))
             finish(s - 2)
             cube_outer(s)
             clamp(s - 1)
             cube_inner(s)
             quantise_basis(s - 1)
-            products(s - 1)
             join_cubes(s)
+            if s < HALVES:
+                spline_weights[s] = quantise_weight("spline%d" % s, spline_grouped[s], SPLINE_FACTORS)
+            products(s - 1)
             quantise_x(s + 1)

@@ -1,3 +1,4 @@
+import math
 from contextlib import ExitStack
 
 import concourse.mybir as mybir
@@ -21,12 +22,16 @@ OUT_TILES = OUTPUTS // P
 PAIR = 2
 ROUND_TILES = [1] * PAIR + [PAIR] * (ROW_TILES // PAIR - 2) + [1] * PAIR
 ROUNDS = len(ROUND_TILES)
+VECTOR_FINISHES = 6
 TILE_GROUPED = P * PACK
 HALVES = 2
 
 LAST_FACTOR = 0.8
 SPLINE_FACTORS = (1.0, 0.25)
 BASE_FACTORS = (0.125,)
+
+OUTER_SCALE = math.sqrt(6.0)
+MIXED_SCALE = math.sqrt(12.0)
 
 
 def turn_rows(nc, turned, identity, rows, tiles):
@@ -78,14 +83,21 @@ def tile_advancedkanlayer_pa_t_kernel(tc, x_norm, spline_weight, base_activation
 
         identity = consts.tile([P, P], F32)
         make_identity(nc, identity[:])
-        minus_two_knots = consts.tile([P, KNOTS], F32)
-        nc.vector.tensor_scalar_mul(out=minus_two_knots[:], in0=knots[:], scalar1=-2.0)
+        minus_knots = consts.tile([P, KNOTS], F32)
+        nc.vector.tensor_scalar_mul(out=minus_knots[:], in0=knots[:], scalar1=-1.0)
         minus_one = consts.tile([P, 1], F32)
         nc.vector.memset(minus_one[:], -1.0)
+        outer_bias = consts.tile([P, 1], F32)
+        nc.vector.tensor_scalar_mul(out=outer_bias[:], in0=minus_one[:], scalar1=OUTER_SCALE)
+        mixed_bias = consts.tile([P, 1], F32)
+        nc.vector.tensor_scalar_mul(out=mixed_bias[:], in0=minus_one[:], scalar1=0.75 * MIXED_SCALE)
 
         turned_x, x_grouped, x_codes, x_scales = {}, {}, {}, {}
-        dist, outer_sq, inner_sq, outer_cube, inner_cube, signed, basis = {}, {}, {}, {}, {}, {}, {}
+        dist, outer_sq, mixed_sq, cube, inner, outer, basis = {}, {}, {}, {}, {}, {}, {}
         basis_codes, basis_scales, acc = {}, {}, {}
+
+        def by_feature(tile):
+            return tile[:].rearrange("p g c -> p c g")
 
         def live(k):
             return 0 <= k < ROUNDS
@@ -100,21 +112,24 @@ def tile_advancedkanlayer_pa_t_kernel(tc, x_norm, spline_weight, base_activation
             if not live(k):
                 return
             grouped = ROUND_TILES[k] * TILE_GROUPED
-            x_grouped[k] = twice.tile([P, grouped], BF16, align_bytes=64, name="x_grouped")
+            x_grouped[k] = thrice.tile([P, grouped], BF16, align_bytes=64, name="x_grouped")
             group_words(nc.scalar.copy, x_grouped[k][:], turned_x[k])
-            dist[k] = twice.tile([P, KNOTS, grouped], F32, name="dist")
+            dist[k] = thrice.tile([P, KNOTS, grouped], F32, name="dist")
             for g in range(KNOTS):
                 nc.scalar.activation(
                     out=dist[k][:, g, :],
                     in_=turned_x[k][:].rearrange("p h r -> p (h r)").bitcast(BF16),
                     func=ACT.Abs,
-                    bias=minus_two_knots[:, g : g + 1],
-                    scale=2.0,
+                    bias=minus_knots[:, g : g + 1],
                 )
-            outer_sq[k] = twice.tile([P, KNOTS, grouped], F32, name="outer_sq")
-            nc.scalar.activation(out=outer_sq[k][:], in_=dist[k][:], func=ACT.Square, bias=minus_one[:], scale=0.5)
-            inner_sq[k] = twice.tile([P, KNOTS, grouped], F32, name="inner_sq")
-            nc.scalar.activation(out=inner_sq[k][:], in_=dist[k][:], func=ACT.Square, bias=minus_one[:], scale=1.0)
+            outer_sq[k] = thrice.tile([P, grouped, KNOTS], F32, name="outer_sq")
+            nc.scalar.activation(
+                out=outer_sq[k][:], in_=by_feature(dist[k]), func=ACT.Square, bias=outer_bias[:], scale=OUTER_SCALE
+            )
+            mixed_sq[k] = thrice.tile([P, grouped, KNOTS], F32, name="mixed_sq")
+            nc.scalar.activation(
+                out=mixed_sq[k][:], in_=by_feature(dist[k]), func=ACT.Square, bias=mixed_bias[:], scale=MIXED_SCALE
+            )
 
         def quantise_x(k):
             if not live(k):
@@ -123,40 +138,40 @@ def tile_advancedkanlayer_pa_t_kernel(tc, x_norm, spline_weight, base_activation
             x_scales[k] = thrice.tile([P, ROUND_TILES[k] * P], U8, align_bytes=64, name="x_scales")
             nc.vector.quantize_mx(out=x_codes[k][:].bitcast(FP8X4), scales=x_scales[k][:], in_=x_grouped[k][:])
 
-        def cube_outer(k):
+        def cubes(k):
             if not live(k):
                 return
-            outer_cube[k] = twice.tile([P, KNOTS, ROUND_TILES[k] * TILE_GROUPED], F32, name="outer_cube")
+            cube[k] = twice.tile([P, ROUND_TILES[k] * TILE_GROUPED, KNOTS], F32, name="cube")
             nc.vector.scalar_tensor_tensor(
-                out=outer_cube[k][:], in0=dist[k][:], scalar=2.0, in1=outer_sq[k][:], op0=ALU.subtract, op1=ALU.mult
+                out=cube[k][:], in0=by_feature(dist[k]), scalar=1.0, in1=outer_sq[k][:], op0=ALU.subtract, op1=ALU.mult
             )
 
-        def cube_inner(k):
+        def inners(k):
             if not live(k):
                 return
-            inner_cube[k] = twice.tile([P, KNOTS, ROUND_TILES[k] * TILE_GROUPED], F32, name="inner_cube")
+            inner[k] = twice.tile([P, ROUND_TILES[k] * TILE_GROUPED, KNOTS], BF16, name="inner")
             nc.vector.scalar_tensor_tensor(
-                out=inner_cube[k][:], in0=dist[k][:], scalar=1.0, in1=inner_sq[k][:], op0=ALU.subtract, op1=ALU.mult
+                out=inner[k][:], in0=mixed_sq[k][:], scalar=0.25, in1=cube[k][:], op0=ALU.add, op1=ALU.add
             )
 
-        def join_cubes(k):
+        def outers(k):
             if not live(k):
                 return
-            signed[k] = twice.tile([P, KNOTS * ROUND_TILES[k] * TILE_GROUPED], BF16, name="signed")
-            nc.vector.scalar_tensor_tensor(
-                out=signed[k][:].rearrange("p (c g) -> p c g", g=KNOTS),
-                in0=inner_cube[k][:].rearrange("p g c -> p c g"),
-                scalar=0.0,
-                in1=outer_cube[k][:].rearrange("p g c -> p c g"),
-                op0=ALU.min,
-                op1=ALU.subtract,
+            outer[k] = twice.tile([P, ROUND_TILES[k] * TILE_GROUPED, KNOTS], BF16, name="outer")
+            nc.vector.tensor_scalar(
+                out=outer[k][:], in0=cube[k][:], scalar1=-1.0 / 3.0, scalar2=0.0, op0=ALU.mult, op1=ALU.max
             )
 
-        def clamp(k):
+        def choose(k):
             if not live(k):
                 return
-            basis[k] = twice.tile([P, KNOTS * ROUND_TILES[k] * TILE_GROUPED], BF16, align_bytes=64, name="basis")
-            nc.vector.tensor_scalar_max(out=basis[k][:], in0=signed[k][:], scalar1=0.0)
+            basis[k] = twice.tile([P, ROUND_TILES[k] * TILE_GROUPED * KNOTS], BF16, align_bytes=64, name="basis")
+            nc.vector.tensor_tensor(
+                out=basis[k][:],
+                in0=inner[k][:].rearrange("p c g -> p (c g)"),
+                in1=outer[k][:].rearrange("p c g -> p (c g)"),
+                op=ALU.min,
+            )
 
         def quantise_basis(k):
             if not live(k):
@@ -197,7 +212,10 @@ def tile_advancedkanlayer_pa_t_kernel(tc, x_norm, spline_weight, base_activation
                 return
             result = thrice.tile([P, ROUND_TILES[k], OUTPUTS], F32, name="result")
             for t in range(ROUND_TILES[k]):
-                nc.scalar.activation(out=result[:, t, :], in_=acc[k, t][:], func=ACT.Copy, scale=LAST_FACTOR)
+                if (tiles_of(k).start + t) % VECTOR_FINISHES == VECTOR_FINISHES - 1:
+                    nc.vector.tensor_scalar_mul(out=result[:, t, :], in0=acc[k, t][:], scalar1=LAST_FACTOR)
+                else:
+                    nc.scalar.activation(out=result[:, t, :], in_=acc[k, t][:], func=ACT.Copy, scale=LAST_FACTOR)
             nc.sync.dma_start(out=out_view[:, tiles_of(k), :], in_=result[:])
 
         def turn_base(turned, c, t):
@@ -237,7 +255,10 @@ def tile_advancedkanlayer_pa_t_kernel(tc, x_norm, spline_weight, base_activation
                 operands.append((codes, scales))
             return operands
 
-        spline_weights, spline_grouped = {}, {}
+        def make_spline(h):
+            return quantise_weight("spline%d" % h, group_weight(nc.vector.tensor_copy, turn_spline(h)), SPLINE_FACTORS)
+
+        spline_weights = {}
 
         turn_x(0)
         scalar_chain(0)
@@ -245,19 +266,18 @@ def tile_advancedkanlayer_pa_t_kernel(tc, x_norm, spline_weight, base_activation
         base_grouped = group_weight(nc.vector.tensor_copy, turn_base)
         base_weights = quantise_weight("base", base_grouped, BASE_FACTORS)
         quantise_x(0)
+        spline_weights[0] = make_spline(0)
 
         for s in range(ROUNDS + 2):
             turn_x(s + 2)
             scalar_chain(s + 1)
-            if s < HALVES:
-                spline_grouped[s] = group_weight(nc.scalar.copy, turn_spline(s))
-            finish(s - 2)
-            cube_outer(s)
-            clamp(s - 1)
-            cube_inner(s)
+            cubes(s)
+            choose(s - 1)
+            inners(s)
             quantise_basis(s - 1)
-            join_cubes(s)
-            if s < HALVES:
-                spline_weights[s] = quantise_weight("spline%d" % s, spline_grouped[s], SPLINE_FACTORS)
+            outers(s)
+            if s == 0:
+                spline_weights[1] = make_spline(1)
             products(s - 1)
+            finish(s - 2)
             quantise_x(s + 1)

@@ -20,18 +20,20 @@ FLOPS = 2 * BATCH * OUTPUTS * (FEATURES * KNOTS + FEATURES)
 ROW_TILES = BATCH // P
 OUT_TILES = OUTPUTS // P
 PAIR = 2
-ROUND_TILES = [1] * PAIR + [PAIR] * (ROW_TILES // PAIR - 2) + [1] * PAIR
-ROUNDS = len(ROUND_TILES)
-VECTOR_FINISHES = 6
-TILE_GROUPED = P * PACK
 HALVES = 2
+ROUNDS = (
+    [(0, 1, 0, HALVES), (1, 1, 0, HALVES)]
+    + [(t, PAIR, 0, HALVES) for t in range(PAIR, ROW_TILES - PAIR, PAIR)]
+    + [(ROW_TILES - 2, 1, 0, HALVES), (ROW_TILES - 1, 1, 0, 1), (ROW_TILES - 1, 1, 1, 1)]
+)
+VECTOR_FINISHES = 10
+TILE_GROUPED = P * PACK
 
-LAST_FACTOR = 0.8
-SPLINE_FACTORS = (1.0, 0.25)
-BASE_FACTORS = (0.125,)
+LAST_FACTOR = 0.1
+SPLINE_FACTORS = (1.0, 4.0)
+BASE_FACTORS = (1.0,)
 
-OUTER_SCALE = math.sqrt(6.0)
-MIXED_SCALE = math.sqrt(12.0)
+ROOT_SIX = math.sqrt(6.0)
 
 
 def turn_rows(nc, turned, identity, rows, tiles):
@@ -63,8 +65,24 @@ def tile_advancedkanlayer_pa_t_kernel(tc, x_norm, spline_weight, base_activation
         stack.enter_context(tc.manual_schedule())
 
         def tiles_of(k):
-            first = sum(ROUND_TILES[:k])
-            return slice(first, first + ROUND_TILES[k])
+            first, count = ROUNDS[k][:2]
+            return range(first, first + count)
+
+        def rows_of(k):
+            return slice(tiles_of(k).start, tiles_of(k).stop)
+
+        def halves_of(k):
+            first, count = ROUNDS[k][2:]
+            return range(first, first + count)
+
+        def opens(k):
+            return halves_of(k).start == 0
+
+        def closes(k):
+            return halves_of(k).stop == HALVES
+
+        def words_of(k):
+            return len(halves_of(k)) * len(tiles_of(k)) * P
 
         x_view = x_norm.rearrange("(p t) i -> p t i", t=ROW_TILES)
         out_view = out.rearrange("(p t) o -> p t o", t=ROW_TILES)
@@ -72,92 +90,117 @@ def tile_advancedkanlayer_pa_t_kernel(tc, x_norm, spline_weight, base_activation
         knots = consts.tile([P, KNOTS], BF16)
         nc.scalar.dma_start(out=knots[:], in_=grid_points.partition_broadcast(P))
         x_rows = consts.tile([P, ROW_TILES, FEATURES], BF16)
-        for k in range(2):
-            nc.sync.dma_start(out=x_rows[:, tiles_of(k), :], in_=x_view[:, tiles_of(k), :])
         a_rows = weights.tile([P, OUT_TILES, FEATURES], BF16)
-        nc.sync.dma_start(out=a_rows[:], in_=base_activation.rearrange("(c p) i -> p c i", p=P))
+        a_view = base_activation.rearrange("(c p) i -> p c i", p=P)
+        for k in range(2):
+            nc.sync.dma_start(out=x_rows[:, rows_of(k), :], in_=x_view[:, rows_of(k), :])
+            part = slice(k * PAIR, (k + 1) * PAIR)
+            nc.sync.dma_start(out=a_rows[:, part, :], in_=a_view[:, part, :])
         w_rows = weights.tile([P, OUT_TILES, FEATURES * KNOTS], BF16)
         nc.sync.dma_start(out=w_rows[:], in_=spline_weight.rearrange("(c p) i g -> p c (i g)", p=P))
-        for k in range(2, ROUNDS):
-            nc.sync.dma_start(out=x_rows[:, tiles_of(k), :], in_=x_view[:, tiles_of(k), :])
+        for k in range(2, len(ROUNDS)):
+            if opens(k):
+                nc.sync.dma_start(out=x_rows[:, rows_of(k), :], in_=x_view[:, rows_of(k), :])
 
         identity = consts.tile([P, P], F32)
         make_identity(nc, identity[:])
-        minus_knots = consts.tile([P, KNOTS], F32)
-        nc.vector.tensor_scalar_mul(out=minus_knots[:], in0=knots[:], scalar1=-1.0)
+        minus_two_knots = consts.tile([P, KNOTS], F32)
+        nc.vector.tensor_scalar_mul(out=minus_two_knots[:], in0=knots[:], scalar1=-2.0)
         minus_one = consts.tile([P, 1], F32)
         nc.vector.memset(minus_one[:], -1.0)
         outer_bias = consts.tile([P, 1], F32)
-        nc.vector.tensor_scalar_mul(out=outer_bias[:], in0=minus_one[:], scalar1=OUTER_SCALE)
+        nc.vector.tensor_scalar_mul(out=outer_bias[:], in0=minus_one[:], scalar1=ROOT_SIX)
         mixed_bias = consts.tile([P, 1], F32)
-        nc.vector.tensor_scalar_mul(out=mixed_bias[:], in0=minus_one[:], scalar1=0.75 * MIXED_SCALE)
+        nc.vector.tensor_scalar_mul(out=mixed_bias[:], in0=minus_one[:], scalar1=1.5 * ROOT_SIX)
 
         turned_x, x_grouped, x_codes, x_scales = {}, {}, {}, {}
         dist, outer_sq, mixed_sq, cube, inner, outer, basis = {}, {}, {}, {}, {}, {}, {}
-        basis_codes, basis_scales, acc = {}, {}, {}
+        basis_codes, basis_scales, acc, result = {}, {}, {}, {}
 
         def by_feature(tile):
             return tile[:].rearrange("p g c -> p c g")
 
         def live(k):
-            return 0 <= k < ROUNDS
+            return 0 <= k < len(ROUNDS)
 
         def turn_x(k):
             if not live(k):
                 return
-            turned_x[k] = turn_psum.tile([P, HALVES, ROUND_TILES[k] * P], F32, name="turned_x")
-            turn_rows(nc, turned_x[k], identity[:], x_rows[:, tiles_of(k), :], ROUND_TILES[k])
+            if not opens(k):
+                turned_x[k] = turned_x[k - 1]
+                return
+            count = len(tiles_of(k))
+            turned_x[k] = turn_psum.tile([P, HALVES, count * P], F32, name="turned_x")
+            turn_rows(nc, turned_x[k], identity[:], x_rows[:, rows_of(k), :], count)
 
-        def scalar_chain(k):
+        def group_x(k):
             if not live(k):
                 return
-            grouped = ROUND_TILES[k] * TILE_GROUPED
-            x_grouped[k] = thrice.tile([P, grouped], BF16, align_bytes=64, name="x_grouped")
+            if not opens(k):
+                x_grouped[k] = x_grouped[k - 1]
+                return
+            x_grouped[k] = thrice.tile([P, len(tiles_of(k)) * TILE_GROUPED], BF16, align_bytes=64, name="x_grouped")
             group_words(nc.scalar.copy, x_grouped[k][:], turned_x[k])
-            dist[k] = thrice.tile([P, KNOTS, grouped], F32, name="dist")
+
+        def distances(k):
+            if not live(k):
+                return
+            rows = len(tiles_of(k)) * P
+            dist[k] = thrice.tile([P, KNOTS, len(halves_of(k)) * rows * 2], F32, name="dist")
+            words = x_grouped[k][:].rearrange("p (r h e) -> p h r e", h=HALVES, e=2)
             for g in range(KNOTS):
                 nc.scalar.activation(
-                    out=dist[k][:, g, :],
-                    in_=turned_x[k][:].rearrange("p h r -> p (h r)").bitcast(BF16),
+                    out=dist[k][:, g, :].rearrange("p (h r e) -> p h r e", r=rows, e=2),
+                    in_=words[:, halves_of(k).start : halves_of(k).stop],
                     func=ACT.Abs,
-                    bias=minus_knots[:, g : g + 1],
+                    bias=minus_two_knots[:, g : g + 1],
+                    scale=2.0,
                 )
-            outer_sq[k] = thrice.tile([P, grouped, KNOTS], F32, name="outer_sq")
+
+        def squares(k):
+            if not live(k):
+                return
+            features = 2 * words_of(k)
+            outer_sq[k] = thrice.tile([P, features, KNOTS], F32, name="outer_sq")
             nc.scalar.activation(
-                out=outer_sq[k][:], in_=by_feature(dist[k]), func=ACT.Square, bias=outer_bias[:], scale=OUTER_SCALE
+                out=outer_sq[k][:], in_=by_feature(dist[k]), func=ACT.Square, bias=outer_bias[:], scale=0.5 * ROOT_SIX
             )
-            mixed_sq[k] = thrice.tile([P, grouped, KNOTS], F32, name="mixed_sq")
+            mixed_sq[k] = thrice.tile([P, features, KNOTS], F32, name="mixed_sq")
             nc.scalar.activation(
-                out=mixed_sq[k][:], in_=by_feature(dist[k]), func=ACT.Square, bias=mixed_bias[:], scale=MIXED_SCALE
+                out=mixed_sq[k][:], in_=by_feature(dist[k]), func=ACT.Square, bias=mixed_bias[:], scale=ROOT_SIX
             )
 
         def quantise_x(k):
-            if not live(k):
+            if not live(k) or not opens(k):
                 return
-            x_codes[k] = thrice.tile([P, ROUND_TILES[k] * P], U32, align_bytes=64, name="x_codes")
-            x_scales[k] = thrice.tile([P, ROUND_TILES[k] * P], U8, align_bytes=64, name="x_scales")
+            rows = len(tiles_of(k)) * P
+            x_codes[k] = thrice.tile([P, rows], U32, align_bytes=64, name="x_codes")
+            x_scales[k] = thrice.tile([P, rows], U8, align_bytes=64, name="x_scales")
             nc.vector.quantize_mx(out=x_codes[k][:].bitcast(FP8X4), scales=x_scales[k][:], in_=x_grouped[k][:])
 
         def cubes(k):
             if not live(k):
                 return
-            cube[k] = twice.tile([P, ROUND_TILES[k] * TILE_GROUPED, KNOTS], F32, name="cube")
+            cube[k] = twice.tile([P, 2 * words_of(k), KNOTS], F32, name="cube")
             nc.vector.scalar_tensor_tensor(
-                out=cube[k][:], in0=by_feature(dist[k]), scalar=1.0, in1=outer_sq[k][:], op0=ALU.subtract, op1=ALU.mult
+                out=cube[k][:], in0=by_feature(dist[k]), scalar=2.0, in1=outer_sq[k][:], op0=ALU.subtract, op1=ALU.mult
             )
 
         def inners(k):
             if not live(k):
                 return
-            inner[k] = twice.tile([P, ROUND_TILES[k] * TILE_GROUPED, KNOTS], BF16, name="inner")
+            inner[k] = twice.tile([P, 2 * words_of(k), KNOTS], BF16, name="inner")
             nc.vector.scalar_tensor_tensor(
-                out=inner[k][:], in0=mixed_sq[k][:], scalar=0.25, in1=cube[k][:], op0=ALU.add, op1=ALU.add
+                out=inner[k][:], in0=mixed_sq[k][:], scalar=0.5, in1=cube[k][:], op0=ALU.add, op1=ALU.add
             )
 
         def outers(k):
             if not live(k):
                 return
-            outer[k] = twice.tile([P, ROUND_TILES[k] * TILE_GROUPED, KNOTS], BF16, name="outer")
+            outer[k] = twice.tile([P, 2 * words_of(k), KNOTS], BF16, name="outer")
+            if k == len(ROUNDS) - 1:
+                nc.scalar.activation(out=outer[k][:], in_=cube[k][:], func=ACT.Relu, scale=-1.0 / 3.0)
+                return
             nc.vector.tensor_scalar(
                 out=outer[k][:], in0=cube[k][:], scalar1=-1.0 / 3.0, scalar2=0.0, op0=ALU.mult, op1=ALU.max
             )
@@ -165,7 +208,7 @@ def tile_advancedkanlayer_pa_t_kernel(tc, x_norm, spline_weight, base_activation
         def choose(k):
             if not live(k):
                 return
-            basis[k] = twice.tile([P, ROUND_TILES[k] * TILE_GROUPED * KNOTS], BF16, align_bytes=64, name="basis")
+            basis[k] = twice.tile([P, PACK * words_of(k)], BF16, align_bytes=64, name="basis")
             nc.vector.tensor_tensor(
                 out=basis[k][:],
                 in0=inner[k][:].rearrange("p c g -> p (c g)"),
@@ -176,8 +219,8 @@ def tile_advancedkanlayer_pa_t_kernel(tc, x_norm, spline_weight, base_activation
         def quantise_basis(k):
             if not live(k):
                 return
-            basis_codes[k] = twice.tile([P, KNOTS * ROUND_TILES[k] * P], U32, align_bytes=64, name="basis_codes")
-            basis_scales[k] = twice.tile([P, KNOTS * ROUND_TILES[k] * P], U8, align_bytes=64, name="basis_scales")
+            basis_codes[k] = twice.tile([P, words_of(k)], U32, align_bytes=64, name="basis_codes")
+            basis_scales[k] = twice.tile([P, words_of(k)], U8, align_bytes=64, name="basis_scales")
             nc.vector.quantize_mx(
                 out=basis_codes[k][:].bitcast(FP8X4), scales=basis_scales[k][:], in_=basis[k][:]
             )
@@ -185,38 +228,47 @@ def tile_advancedkanlayer_pa_t_kernel(tc, x_norm, spline_weight, base_activation
         def products(k):
             if not live(k):
                 return
-            for t in range(ROUND_TILES[k]):
+            for t, tile in enumerate(tiles_of(k)):
                 passes = []
-                for moving in base_weights:
+                if opens(k):
+                    acc[tile] = acc_psum.tile([P, OUTPUTS], F32, name="acc")
                     cols = slice(t * P, (t + 1) * P)
-                    passes.append((x_codes[k][:, cols], x_scales[k][:, cols], moving))
-                for h in range(HALVES):
-                    first = (h * ROUND_TILES[k] + t) * P
+                    for moving in base_weights:
+                        passes.append((x_codes[k][:, cols], x_scales[k][:, cols], moving))
+                for h in halves_of(k):
+                    first = ((h - halves_of(k).start) * len(tiles_of(k)) + t) * P
                     cols = slice(first, first + P)
                     for moving in spline_weights[h]:
                         passes.append((basis_codes[k][:, cols], basis_scales[k][:, cols], moving))
-                acc[k, t] = acc_psum.tile([P, OUTPUTS], F32, name="acc")
                 for n, (codes, scales, moving) in enumerate(passes):
                     nc.tensor.matmul_mx(
-                        out=acc[k, t][:],
+                        out=acc[tile][:],
                         lhsT=codes.bitcast(FP8X4),
                         lhsT_scale=scales,
                         rhs=moving[0][:].bitcast(FP8X4),
                         rhs_scale=moving[1][:],
-                        start=(n == 0),
-                        stop=(n == len(passes) - 1),
+                        start=(opens(k) and n == 0),
+                        stop=(closes(k) and n == len(passes) - 1),
                     )
 
-        def finish(k):
-            if not live(k):
+        def on_vector(tile):
+            return tile % VECTOR_FINISHES == VECTOR_FINISHES // 2
+
+        def finish_on_scalar(k):
+            if not live(k) or not closes(k):
                 return
-            result = thrice.tile([P, ROUND_TILES[k], OUTPUTS], F32, name="result")
-            for t in range(ROUND_TILES[k]):
-                if (tiles_of(k).start + t) % VECTOR_FINISHES == VECTOR_FINISHES - 1:
-                    nc.vector.tensor_scalar_mul(out=result[:, t, :], in0=acc[k, t][:], scalar1=LAST_FACTOR)
-                else:
-                    nc.scalar.activation(out=result[:, t, :], in_=acc[k, t][:], func=ACT.Copy, scale=LAST_FACTOR)
-            nc.sync.dma_start(out=out_view[:, tiles_of(k), :], in_=result[:])
+            result[k] = thrice.tile([P, len(tiles_of(k)), OUTPUTS], F32, name="result")
+            for t, tile in enumerate(tiles_of(k)):
+                if not on_vector(tile):
+                    nc.scalar.activation(out=result[k][:, t, :], in_=acc[tile][:], func=ACT.Copy, scale=LAST_FACTOR)
+
+        def finish(k):
+            if not live(k) or not closes(k):
+                return
+            for t, tile in enumerate(tiles_of(k)):
+                if on_vector(tile):
+                    nc.vector.tensor_scalar_mul(out=result[k][:, t, :], in0=acc[tile][:], scalar1=LAST_FACTOR)
+            nc.sync.dma_start(out=out_view[:, rows_of(k), :], in_=result[k][:])
 
         def turn_base(turned, c, t):
             turn_rows(nc, turned[:, :, t * P : (t + 1) * P], identity[:], a_rows[:, c : c + 1, :], 1)
@@ -261,16 +313,22 @@ def tile_advancedkanlayer_pa_t_kernel(tc, x_norm, spline_weight, base_activation
         spline_weights = {}
 
         turn_x(0)
-        scalar_chain(0)
+        group_x(0)
+        distances(0)
         turn_x(1)
+        group_x(1)
+        squares(0)
         base_grouped = group_weight(nc.vector.tensor_copy, turn_base)
         base_weights = quantise_weight("base", base_grouped, BASE_FACTORS)
         quantise_x(0)
         spline_weights[0] = make_spline(0)
+        turn_x(2)
 
-        for s in range(ROUNDS + 2):
-            turn_x(s + 2)
-            scalar_chain(s + 1)
+        for s in range(len(ROUNDS) + 2):
+            distances(s + 1)
+            group_x(s + 2)
+            squares(s + 1)
+            finish_on_scalar(s - 2)
             cubes(s)
             choose(s - 1)
             inners(s)
@@ -278,6 +336,7 @@ def tile_advancedkanlayer_pa_t_kernel(tc, x_norm, spline_weight, base_activation
             outers(s)
             if s == 0:
                 spline_weights[1] = make_spline(1)
+            turn_x(s + 3)
             products(s - 1)
             finish(s - 2)
             quantise_x(s + 1)

@@ -88,7 +88,8 @@ def tile_advancedkanlayer_pa_t_kernel(tc, x_norm, spline_weight, base_activation
         out_view = out.rearrange("(p t) o -> p t o", t=ROW_TILES)
 
         knots = consts.tile([P, KNOTS], BF16)
-        nc.scalar.dma_start(out=knots[:], in_=grid_points.partition_broadcast(P))
+        nc.vector.memset(knots[:], 0.0)
+        nc.scalar.dma_start(out=knots[:1, :], in_=grid_points.rearrange("(o g) -> o g", o=1))
         x_rows = consts.tile([P, ROW_TILES, FEATURES], BF16)
         a_rows = weights.tile([P, OUT_TILES, FEATURES], BF16)
         a_view = base_activation.rearrange("(c p) i -> p c i", p=P)
@@ -104,8 +105,8 @@ def tile_advancedkanlayer_pa_t_kernel(tc, x_norm, spline_weight, base_activation
 
         identity = consts.tile([P, P], F32)
         make_identity(nc, identity[:])
-        minus_two_knots = consts.tile([P, KNOTS], F32)
-        nc.vector.tensor_scalar_mul(out=minus_two_knots[:], in0=knots[:], scalar1=-2.0)
+        ones = consts.tile([P, P], BF16)
+        nc.vector.memset(ones[:], 1.0)
         minus_one = consts.tile([P, 1], F32)
         nc.vector.memset(minus_one[:], -1.0)
         outer_bias = consts.tile([P, 1], F32)
@@ -133,14 +134,14 @@ def tile_advancedkanlayer_pa_t_kernel(tc, x_norm, spline_weight, base_activation
             turned_x[k] = turn_psum.tile([P, HALVES, count * P], F32, name="turned_x")
             turn_rows(nc, turned_x[k], identity[:], x_rows[:, rows_of(k), :], count)
 
-        def group_x(k):
+        def group_x(k, copy):
             if not live(k):
                 return
             if not opens(k):
                 x_grouped[k] = x_grouped[k - 1]
                 return
             x_grouped[k] = thrice.tile([P, len(tiles_of(k)) * TILE_GROUPED], BF16, align_bytes=64, name="x_grouped")
-            group_words(nc.scalar.copy, x_grouped[k][:], turned_x[k])
+            group_words(copy, x_grouped[k][:], turned_x[k])
 
         def distances(k):
             if not live(k):
@@ -198,7 +199,7 @@ def tile_advancedkanlayer_pa_t_kernel(tc, x_norm, spline_weight, base_activation
             if not live(k):
                 return
             outer[k] = twice.tile([P, 2 * words_of(k), KNOTS], BF16, name="outer")
-            if k == len(ROUNDS) - 1:
+            if not (opens(k) and closes(k)):
                 nc.scalar.activation(out=outer[k][:], in_=cube[k][:], func=ACT.Relu, scale=-1.0 / 3.0)
                 return
             nc.vector.tensor_scalar(
@@ -312,11 +313,16 @@ def tile_advancedkanlayer_pa_t_kernel(tc, x_norm, spline_weight, base_activation
 
         spline_weights = {}
 
+        spread = turn_psum.tile([P, HALVES, PAIR * P], F32, name="turned_w")
+        nc.tensor.matmul(out=spread[:, 0, :KNOTS], lhsT=ones[:], rhs=knots[:], start=True, stop=True)
+        minus_two_knots = consts.tile([P, KNOTS], F32)
+        nc.vector.tensor_scalar_mul(out=minus_two_knots[:], in0=spread[:, 0, :KNOTS], scalar1=-2.0)
+
         turn_x(0)
-        group_x(0)
+        group_x(0, nc.vector.tensor_copy)
         distances(0)
         turn_x(1)
-        group_x(1)
+        group_x(1, nc.vector.tensor_copy)
         squares(0)
         base_grouped = group_weight(nc.vector.tensor_copy, turn_base)
         base_weights = quantise_weight("base", base_grouped, BASE_FACTORS)
@@ -326,14 +332,14 @@ def tile_advancedkanlayer_pa_t_kernel(tc, x_norm, spline_weight, base_activation
 
         for s in range(len(ROUNDS) + 2):
             distances(s + 1)
-            group_x(s + 2)
+            group_x(s + 2, nc.scalar.copy)
             squares(s + 1)
-            finish_on_scalar(s - 2)
             cubes(s)
             choose(s - 1)
             inners(s)
             quantise_basis(s - 1)
             outers(s)
+            finish_on_scalar(s - 2)
             if s == 0:
                 spline_weights[1] = make_spline(1)
             turn_x(s + 3)

@@ -226,13 +226,18 @@ def tile_advancedkanlayer_pa_t_kernel(tc, x_norm, spline_weight, base_activation
                 out=basis_codes[k][:].bitcast(FP8X4), scales=basis_scales[k][:], in_=basis[k][:]
             )
 
+        def groups_of(tile):
+            width = OUTPUTS // 2 if tile == ROW_TILES - 1 else OUTPUTS
+            return [slice(first, first + width) for first in range(0, OUTPUTS, width)]
+
         def products(k):
             if not live(k):
                 return
             for t, tile in enumerate(tiles_of(k)):
                 passes = []
                 if opens(k):
-                    acc[tile] = acc_psum.tile([P, OUTPUTS], F32, name="acc")
+                    for outputs in groups_of(tile):
+                        acc[tile, outputs.start] = acc_psum.tile([P, OUTPUTS], F32, name="acc")
                     cols = slice(t * P, (t + 1) * P)
                     for moving in base_weights:
                         passes.append((x_codes[k][:, cols], x_scales[k][:, cols], moving))
@@ -241,35 +246,45 @@ def tile_advancedkanlayer_pa_t_kernel(tc, x_norm, spline_weight, base_activation
                     cols = slice(first, first + P)
                     for moving in spline_weights[h]:
                         passes.append((basis_codes[k][:, cols], basis_scales[k][:, cols], moving))
-                for n, (codes, scales, moving) in enumerate(passes):
-                    nc.tensor.matmul_mx(
-                        out=acc[tile][:],
-                        lhsT=codes.bitcast(FP8X4),
-                        lhsT_scale=scales,
-                        rhs=moving[0][:].bitcast(FP8X4),
-                        rhs_scale=moving[1][:],
-                        start=(opens(k) and n == 0),
-                        stop=(closes(k) and n == len(passes) - 1),
-                    )
+                for outputs in groups_of(tile):
+                    for n, (codes, scales, moving) in enumerate(passes):
+                        nc.tensor.matmul_mx(
+                            out=acc[tile, outputs.start][:, : outputs.stop - outputs.start],
+                            lhsT=codes.bitcast(FP8X4),
+                            lhsT_scale=scales,
+                            rhs=moving[0][:, outputs].bitcast(FP8X4),
+                            rhs_scale=moving[1][:, outputs],
+                            start=(opens(k) and n == 0),
+                            stop=(closes(k) and n == len(passes) - 1),
+                        )
 
-        def on_vector(tile):
-            return tile % VECTOR_FINISHES == VECTOR_FINISHES // 2
-
-        def finish_on_scalar(k):
+        def finish(k, part):
             if not live(k) or not closes(k):
                 return
-            result[k] = thrice.tile([P, len(tiles_of(k)), OUTPUTS], F32, name="result")
-            for t, tile in enumerate(tiles_of(k)):
-                if not on_vector(tile):
-                    nc.scalar.activation(out=result[k][:, t, :], in_=acc[tile][:], func=ACT.Copy, scale=LAST_FACTOR)
-
-        def finish(k):
-            if not live(k) or not closes(k):
+            first = tiles_of(k).start
+            if first == ROW_TILES - 1:
+                if part == "vector":
+                    return
+                for n, outputs in enumerate(groups_of(first)):
+                    columns = acc[first, outputs.start][:, : outputs.stop - outputs.start]
+                    half = thrice.tile([P, outputs.stop - outputs.start], F32, name="half%d" % n)
+                    if n == 0:
+                        nc.scalar.activation(out=half[:], in_=columns, func=ACT.Copy, scale=LAST_FACTOR)
+                        nc.scalar.dma_start(out=out_view[:, first, outputs], in_=half[:])
+                    else:
+                        nc.vector.tensor_scalar_mul(out=half[:], in0=columns, scalar1=LAST_FACTOR)
+                        nc.sync.dma_start(out=out_view[:, first, outputs], in_=half[:])
                 return
+            if part == "scalar":
+                result[k] = thrice.tile([P, len(tiles_of(k)), OUTPUTS], F32, name="result")
             for t, tile in enumerate(tiles_of(k)):
-                if on_vector(tile):
-                    nc.vector.tensor_scalar_mul(out=result[k][:, t, :], in0=acc[tile][:], scalar1=LAST_FACTOR)
-            nc.sync.dma_start(out=out_view[:, rows_of(k), :], in_=result[k][:])
+                on_vector = tile % VECTOR_FINISHES == VECTOR_FINISHES // 2
+                if part == "vector" and on_vector:
+                    nc.vector.tensor_scalar_mul(out=result[k][:, t, :], in0=acc[tile, 0][:], scalar1=LAST_FACTOR)
+                if part == "scalar" and not on_vector:
+                    nc.scalar.activation(out=result[k][:, t, :], in_=acc[tile, 0][:], func=ACT.Copy, scale=LAST_FACTOR)
+            if part == "vector":
+                nc.sync.dma_start(out=out_view[:, rows_of(k), :], in_=result[k][:])
 
         def turn_base(turned, c, t):
             turn_rows(nc, turned[:, :, t * P : (t + 1) * P], identity[:], a_rows[:, c : c + 1, :], 1)
@@ -313,16 +328,15 @@ def tile_advancedkanlayer_pa_t_kernel(tc, x_norm, spline_weight, base_activation
 
         spline_weights = {}
 
+        turn_x(0)
         spread = turn_psum.tile([P, HALVES, PAIR * P], F32, name="turned_w")
         nc.tensor.matmul(out=spread[:, 0, :KNOTS], lhsT=ones[:], rhs=knots[:], start=True, stop=True)
         minus_two_knots = consts.tile([P, KNOTS], F32)
         nc.vector.tensor_scalar_mul(out=minus_two_knots[:], in0=spread[:, 0, :KNOTS], scalar1=-2.0)
-
-        turn_x(0)
-        group_x(0, nc.vector.tensor_copy)
-        distances(0)
         turn_x(1)
+        group_x(0, nc.scalar.copy)
         group_x(1, nc.vector.tensor_copy)
+        distances(0)
         squares(0)
         base_grouped = group_weight(nc.vector.tensor_copy, turn_base)
         base_weights = quantise_weight("base", base_grouped, BASE_FACTORS)
@@ -339,10 +353,10 @@ def tile_advancedkanlayer_pa_t_kernel(tc, x_norm, spline_weight, base_activation
             inners(s)
             quantise_basis(s - 1)
             outers(s)
-            finish_on_scalar(s - 2)
+            finish(s - 2, "scalar")
             if s == 0:
                 spline_weights[1] = make_spline(1)
             turn_x(s + 3)
             products(s - 1)
-            finish(s - 2)
+            finish(s - 2, "vector")
             quantise_x(s + 1)

@@ -341,7 +341,6 @@ def tile_advancedkanlayer_pa_t_kernel(tc, x_norm, spline_weight, base_activation
         base_grouped = group_weight(nc.vector.tensor_copy, turn_base)
         base_weights = quantise_weight("base", base_grouped, BASE_FACTORS)
         quantise_x(0)
-        spline_weights[0] = make_spline(0)
         turn_x(2)
 
         for s in range(len(ROUNDS) + 2):
@@ -354,8 +353,8 @@ def tile_advancedkanlayer_pa_t_kernel(tc, x_norm, spline_weight, base_activation
             quantise_basis(s - 1)
             outers(s)
             finish(s - 2, "scalar")
-            if s == 0:
-                spline_weights[1] = make_spline(1)
+            if s < HALVES:
+                spline_weights[s] = make_spline(s)
             turn_x(s + 3)
             products(s - 1)
             finish(s - 2, "vector")

@@ -26,6 +26,7 @@ ROUNDS = (
     + [(t, PAIR, 0, HALVES) for t in range(PAIR, ROW_TILES - PAIR, PAIR)]
     + [(ROW_TILES - 2, 1, 0, HALVES), (ROW_TILES - 1, 1, 0, 1), (ROW_TILES - 1, 1, 1, 1)]
 )
+SUMMED = list(range(2, len(ROUNDS) - 3, 2))
 VECTOR_FINISHES = 10
 TILE_GROUPED = P * PACK
 
@@ -60,8 +61,8 @@ def tile_advancedkanlayer_pa_t_kernel(tc, x_norm, spline_weight, base_activation
         weights = stack.enter_context(tc.tile_pool(name="weights", bufs=1))
         twice = stack.enter_context(tc.tile_pool(name="twice", bufs=2))
         thrice = stack.enter_context(tc.tile_pool(name="thrice", bufs=3))
-        turn_psum = stack.enter_context(tc.psum_pool(name="turn_psum", bufs=2))
-        acc_psum = stack.enter_context(tc.psum_pool(name="acc_psum", bufs=2 * PAIR))
+        bank_psum = stack.enter_context(tc.psum_pool(name="bank_psum", bufs=6))
+        acc_psum = stack.enter_context(tc.psum_pool(name="acc_psum", bufs=PAIR))
         stack.enter_context(tc.manual_schedule())
 
         def tiles_of(k):
@@ -109,6 +110,8 @@ def tile_advancedkanlayer_pa_t_kernel(tc, x_norm, spline_weight, base_activation
         nc.vector.memset(ones[:], 1.0)
         minus_one = consts.tile([P, 1], F32)
         nc.vector.memset(minus_one[:], -1.0)
+        minus_ten = consts.tile([P, 1], F32)
+        nc.vector.memset(minus_ten[:], -10.0)
         outer_bias = consts.tile([P, 1], F32)
         nc.vector.tensor_scalar_mul(out=outer_bias[:], in0=minus_one[:], scalar1=ROOT_SIX)
         mixed_bias = consts.tile([P, 1], F32)
@@ -117,6 +120,7 @@ def tile_advancedkanlayer_pa_t_kernel(tc, x_norm, spline_weight, base_activation
         turned_x, x_grouped, x_codes, x_scales = {}, {}, {}, {}
         dist, outer_sq, mixed_sq, cube, inner, outer, basis = {}, {}, {}, {}, {}, {}, {}
         basis_codes, basis_scales, acc, result = {}, {}, {}, {}
+        sums, turned_outer = {}, {}
 
         def by_feature(tile):
             return tile[:].rearrange("p g c -> p c g")
@@ -131,7 +135,7 @@ def tile_advancedkanlayer_pa_t_kernel(tc, x_norm, spline_weight, base_activation
                 turned_x[k] = turned_x[k - 1]
                 return
             count = len(tiles_of(k))
-            turned_x[k] = turn_psum.tile([P, HALVES, count * P], F32, name="turned_x")
+            turned_x[k] = bank_psum.tile([P, HALVES, count * P], F32, name="bank")
             turn_rows(nc, turned_x[k], identity[:], x_rows[:, rows_of(k), :], count)
 
         def group_x(k, copy):
@@ -145,6 +149,17 @@ def tile_advancedkanlayer_pa_t_kernel(tc, x_norm, spline_weight, base_activation
 
         def distances(k):
             if not live(k):
+                return
+            if k in SUMMED:
+                dist[k] = thrice.tile([P, KNOTS, len(tiles_of(k)) * FEATURES], F32, name="dist")
+                for g in range(KNOTS):
+                    nc.scalar.activation(
+                        out=dist[k][:, g, :].rearrange("r (b e p) -> r b e p", e=2, p=P),
+                        in_=x_rows[:, rows_of(k), :].rearrange("r t (h p e) -> r (t h) e p", h=HALVES, e=2),
+                        func=ACT.Abs,
+                        bias=minus_half_knots[:, g : g + 1],
+                        scale=0.5,
+                    )
                 return
             rows = len(tiles_of(k)) * P
             dist[k] = thrice.tile([P, KNOTS, len(halves_of(k)) * rows * 2], F32, name="dist")
@@ -162,6 +177,12 @@ def tile_advancedkanlayer_pa_t_kernel(tc, x_norm, spline_weight, base_activation
             if not live(k):
                 return
             features = 2 * words_of(k)
+            if k in SUMMED:
+                outer_sq[k] = thrice.tile([P, KNOTS, features], F32, name="outer_sq")
+                nc.scalar.activation(
+                    out=outer_sq[k][:], in_=dist[k][:], func=ACT.Square, bias=minus_one[:], scale=2.0
+                )
+                return
             outer_sq[k] = thrice.tile([P, features, KNOTS], F32, name="outer_sq")
             nc.scalar.activation(
                 out=outer_sq[k][:], in_=by_feature(dist[k]), func=ACT.Square, bias=outer_bias[:], scale=0.5 * ROOT_SIX
@@ -182,6 +203,12 @@ def tile_advancedkanlayer_pa_t_kernel(tc, x_norm, spline_weight, base_activation
         def cubes(k):
             if not live(k):
                 return
+            if k in SUMMED:
+                cube[k] = twice.tile([P, KNOTS, 2 * words_of(k)], F32, name="cube")
+                nc.vector.scalar_tensor_tensor(
+                    out=cube[k][:], in0=dist[k][:], scalar=0.5, in1=outer_sq[k][:], op0=ALU.subtract, op1=ALU.mult
+                )
+                return
             cube[k] = twice.tile([P, 2 * words_of(k), KNOTS], F32, name="cube")
             nc.vector.scalar_tensor_tensor(
                 out=cube[k][:], in0=by_feature(dist[k]), scalar=2.0, in1=outer_sq[k][:], op0=ALU.subtract, op1=ALU.mult
@@ -189,6 +216,8 @@ def tile_advancedkanlayer_pa_t_kernel(tc, x_norm, spline_weight, base_activation
 
         def inners(k):
             if not live(k):
+                return
+            if k in SUMMED:
                 return
             inner[k] = twice.tile([P, 2 * words_of(k), KNOTS], BF16, name="inner")
             nc.vector.scalar_tensor_tensor(
@@ -199,6 +228,11 @@ def tile_advancedkanlayer_pa_t_kernel(tc, x_norm, spline_weight, base_activation
             if not live(k):
                 return
             outer[k] = twice.tile([P, 2 * words_of(k), KNOTS], BF16, name="outer")
+            if k in SUMMED:
+                nc.vector.tensor_scalar(
+                    out=outer[k][:], in0=by_feature(cube[k]), scalar1=-8.0, scalar2=0.0, op0=ALU.mult, op1=ALU.max
+                )
+                return
             if not (opens(k) and closes(k)):
                 nc.scalar.activation(out=outer[k][:], in_=cube[k][:], func=ACT.Relu, scale=-1.0 / 3.0)
                 return
@@ -206,10 +240,76 @@ def tile_advancedkanlayer_pa_t_kernel(tc, x_norm, spline_weight, base_activation
                 out=outer[k][:], in0=cube[k][:], scalar1=-1.0 / 3.0, scalar2=0.0, op0=ALU.mult, op1=ALU.max
             )
 
+        def block(tile, k, t, h, e):
+            first = ((t * HALVES + h) * 2 + e) * P
+            return tile[:, first : first + P]
+
+        def sum_terms(k):
+            if not live(k) or k not in SUMMED:
+                return
+            for t in range(len(tiles_of(k))):
+                for h in range(HALVES):
+                    sums[k, t, h] = bank_psum.tile([P, PACK, P], F32, name="bank")
+                    for e in range(2):
+                        for g in range(KNOTS):
+                            terms = [outer_sq[k], dist[k], cube[k]]
+                            for n, term in enumerate(terms):
+                                nc.tensor.matmul(
+                                    out=sums[k, t, h][:, 2 * e + g, :],
+                                    lhsT=block(term[:, g, :], k, t, h, e),
+                                    rhs=identity[:],
+                                    is_transpose=True,
+                                    start=(n == 0),
+                                    stop=(n == len(terms) - 1),
+                                )
+
+        def turn_outer(k):
+            if not live(k) or k not in SUMMED:
+                return
+            for t in range(len(tiles_of(k))):
+                turned_outer[k, t] = bank_psum.tile([P, HALVES, 2, P], F32, name="bank")
+                words = outer[k][:].rearrange("r c g -> r (c g)").bitcast(F32)
+                for h in range(HALVES):
+                    for e in range(2):
+                        nc.tensor.transpose(
+                            out=turned_outer[k, t][:, h, e, :], in_=block(words, k, t, h, e), identity=identity[:]
+                        )
+
+        def leave(k, h):
+            if not live(k) or k not in SUMMED:
+                return
+            count = len(tiles_of(k))
+            if h == 0:
+                inner[k] = twice.tile([P, PACK * words_of(k)], BF16, name="inner")
+            for t in range(count):
+                first = (h * count + t) * P * PACK
+                place = inner[k][:, first : first + P * PACK].rearrange("p (r b) -> p r b", b=PACK)
+                source = sums[k, t, h][:].rearrange("p b r -> p r b")
+                if h == 0:
+                    nc.scalar.activation(out=place, in_=source, func=ACT.Identity, bias=minus_ten[:], scale=24.0)
+                else:
+                    nc.vector.tensor_scalar(
+                        out=place, in0=source, scalar1=24.0, scalar2=-10.0, op0=ALU.mult, op1=ALU.add
+                    )
+
         def choose(k):
             if not live(k):
                 return
             basis[k] = twice.tile([P, PACK * words_of(k)], BF16, align_bytes=64, name="basis")
+            if k in SUMMED:
+                count = len(tiles_of(k))
+                for t in range(count):
+                    for h in range(HALVES):
+                        first = (h * count + t) * P * PACK
+                        cols = slice(first, first + P * PACK)
+                        words = turned_outer[k, t][:, h].rearrange("p e r -> p (e r)").bitcast(BF16)
+                        nc.vector.tensor_tensor(
+                            out=basis[k][:, cols].rearrange("p (r e g) -> p r e g", e=2, g=KNOTS),
+                            in0=inner[k][:, cols].rearrange("p (r e g) -> p r e g", e=2, g=KNOTS),
+                            in1=words.rearrange("p (e r g) -> p r e g", e=2, g=KNOTS),
+                            op=ALU.min,
+                        )
+                return
             nc.vector.tensor_tensor(
                 out=basis[k][:],
                 in0=inner[k][:].rearrange("p c g -> p (c g)"),
@@ -303,7 +403,7 @@ def tile_advancedkanlayer_pa_t_kernel(tc, x_norm, spline_weight, base_activation
         def group_weight(copy, turn):
             grouped = twice.tile([P, OUTPUTS * PACK], BF16, align_bytes=64, name="w_grouped")
             for pair in range(OUT_TILES // PAIR):
-                turned_w = turn_psum.tile([P, HALVES, PAIR * P], F32, name="turned_w")
+                turned_w = bank_psum.tile([P, HALVES, PAIR * P], F32, name="bank")
                 for t in range(PAIR):
                     turn(turned_w, pair * PAIR + t, t)
                 columns = slice(pair * PAIR * TILE_GROUPED, (pair + 1) * PAIR * TILE_GROUPED)
@@ -329,10 +429,12 @@ def tile_advancedkanlayer_pa_t_kernel(tc, x_norm, spline_weight, base_activation
         spline_weights = {}
 
         turn_x(0)
-        spread = turn_psum.tile([P, HALVES, PAIR * P], F32, name="turned_w")
+        spread = bank_psum.tile([P, HALVES, PAIR * P], F32, name="bank")
         nc.tensor.matmul(out=spread[:, 0, :KNOTS], lhsT=ones[:], rhs=knots[:], start=True, stop=True)
         minus_two_knots = consts.tile([P, KNOTS], F32)
         nc.vector.tensor_scalar_mul(out=minus_two_knots[:], in0=spread[:, 0, :KNOTS], scalar1=-2.0)
+        minus_half_knots = consts.tile([P, KNOTS], F32)
+        nc.vector.tensor_scalar_mul(out=minus_half_knots[:], in0=spread[:, 0, :KNOTS], scalar1=-0.5)
         turn_x(1)
         group_x(0, nc.scalar.copy)
         group_x(1, nc.vector.tensor_copy)
@@ -345,17 +447,27 @@ def tile_advancedkanlayer_pa_t_kernel(tc, x_norm, spline_weight, base_activation
 
         for s in range(len(ROUNDS) + 2):
             distances(s + 1)
+            leave(s - 1, 0)
             group_x(s + 2, nc.scalar.copy)
             squares(s + 1)
             cubes(s)
-            choose(s - 1)
+            leave(s - 1, 1)
+            if s - 1 not in SUMMED:
+                choose(s - 1)
             inners(s)
-            quantise_basis(s - 1)
+            if s - 1 not in SUMMED:
+                quantise_basis(s - 1)
             outers(s)
+            if s - 1 in SUMMED:
+                choose(s - 1)
             finish(s - 2, "scalar")
             if s < HALVES:
                 spline_weights[s] = make_spline(s)
             turn_x(s + 3)
+            quantise_x(s + 1)
+            if s - 1 in SUMMED:
+                quantise_basis(s - 1)
+            sum_terms(s)
+            turn_outer(s)
             products(s - 1)
             finish(s - 2, "vector")
-            quantise_x(s + 1)

@@ -267,21 +267,21 @@ def tile_advancedkanlayer_pa_t_kernel(tc, x_norm, spline_weight, base_activation
             if not live(k) or k not in SUMMED:
                 return
             for t in range(len(tiles_of(k))):
-                turned_outer[k, t] = bank_psum.tile([P, HALVES, 2, P], F32, name="bank")
+                turned_outer[k, t] = bank_psum.tile([P, HALVES, P, 2], F32, name="bank")
                 words = outer[k][:].rearrange("r c g -> r (c g)").bitcast(F32)
                 for h in range(HALVES):
                     for e in range(2):
                         nc.tensor.transpose(
-                            out=turned_outer[k, t][:, h, e, :], in_=block(words, k, t, h, e), identity=identity[:]
+                            out=turned_outer[k, t][:, h, :, e], in_=block(words, k, t, h, e), identity=identity[:]
                         )
 
-        def leave(k, h):
+        def leave(k, h, tiles):
             if not live(k) or k not in SUMMED:
                 return
             count = len(tiles_of(k))
-            if h == 0:
+            if k not in inner:
                 inner[k] = twice.tile([P, PACK * words_of(k)], BF16, name="inner")
-            for t in range(count):
+            for t in tiles:
                 first = (h * count + t) * P * PACK
                 place = inner[k][:, first : first + P * PACK].rearrange("p (r b) -> p r b", b=PACK)
                 source = sums[k, t, h][:].rearrange("p b r -> p r b")
@@ -299,16 +299,12 @@ def tile_advancedkanlayer_pa_t_kernel(tc, x_norm, spline_weight, base_activation
             if k in SUMMED:
                 count = len(tiles_of(k))
                 for t in range(count):
-                    for h in range(HALVES):
-                        first = (h * count + t) * P * PACK
-                        cols = slice(first, first + P * PACK)
-                        words = turned_outer[k, t][:, h].rearrange("p e r -> p (e r)").bitcast(BF16)
-                        nc.vector.tensor_tensor(
-                            out=basis[k][:, cols].rearrange("p (r e g) -> p r e g", e=2, g=KNOTS),
-                            in0=inner[k][:, cols].rearrange("p (r e g) -> p r e g", e=2, g=KNOTS),
-                            in1=words.rearrange("p (e r g) -> p r e g", e=2, g=KNOTS),
-                            op=ALU.min,
-                        )
+                    nc.vector.tensor_tensor(
+                        out=basis[k][:].rearrange("p (h t c) -> p t h c", h=HALVES, t=count)[:, t],
+                        in0=inner[k][:].rearrange("p (h t c) -> p t h c", h=HALVES, t=count)[:, t],
+                        in1=turned_outer[k, t][:].rearrange("p h r e -> p h (r e)").bitcast(BF16),
+                        op=ALU.min,
+                    )
                 return
             nc.vector.tensor_tensor(
                 out=basis[k][:],
@@ -447,11 +443,11 @@ def tile_advancedkanlayer_pa_t_kernel(tc, x_norm, spline_weight, base_activation
 
         for s in range(len(ROUNDS) + 2):
             distances(s + 1)
-            leave(s - 1, 0)
+            leave(s - 1, 0, (0, 1))
             group_x(s + 2, nc.scalar.copy)
             squares(s + 1)
             cubes(s)
-            leave(s - 1, 1)
+            leave(s - 1, 1, (0, 1))
             if s - 1 not in SUMMED:
                 choose(s - 1)
             inners(s)

@@ -26,7 +26,7 @@ ROUNDS = (
     + [(t, PAIR, 0, HALVES) for t in range(PAIR, ROW_TILES - PAIR, PAIR)]
     + [(ROW_TILES - 2, 1, 0, HALVES), (ROW_TILES - 1, 1, 0, 1), (ROW_TILES - 1, 1, 1, 1)]
 )
-SUMMED = list(range(2, len(ROUNDS) - 3, 2))
+SUMMED = [k for k in range(2, len(ROUNDS) - 3) if k % 3 != 0]
 VECTOR_FINISHES = 10
 TILE_GROUPED = P * PACK
 
@@ -447,10 +447,11 @@ def tile_advancedkanlayer_pa_t_kernel(tc, x_norm, spline_weight, base_activation
             group_x(s + 2, nc.scalar.copy)
             squares(s + 1)
             cubes(s)
-            leave(s - 1, 1, (0, 1))
+            leave(s - 1, 1, (0,))
             if s - 1 not in SUMMED:
                 choose(s - 1)
             inners(s)
+            leave(s - 1, 1, (1,))
             if s - 1 not in SUMMED:
                 quantise_basis(s - 1)
             outers(s)

@@ -26,7 +26,7 @@ ROUNDS = (
     + [(t, PAIR, 0, HALVES) for t in range(PAIR, ROW_TILES - PAIR, PAIR)]
     + [(ROW_TILES - 2, 1, 0, HALVES), (ROW_TILES - 1, 1, 0, 1), (ROW_TILES - 1, 1, 1, 1)]
 )
-SUMMED = [k for k in range(2, len(ROUNDS) - 3) if k % 3 != 0]
+SUMMED = [k for k in range(len(ROUNDS) - 3) if k < 2 or k % 3 != 0]
 VECTOR_FINISHES = 10
 TILE_GROUPED = P * PACK
 
@@ -94,15 +94,15 @@ def tile_advancedkanlayer_pa_t_kernel(tc, x_norm, spline_weight, base_activation
         x_rows = consts.tile([P, ROW_TILES, FEATURES], BF16)
         a_rows = weights.tile([P, OUT_TILES, FEATURES], BF16)
         a_view = base_activation.rearrange("(c p) i -> p c i", p=P)
-        for k in range(2):
-            nc.sync.dma_start(out=x_rows[:, rows_of(k), :], in_=x_view[:, rows_of(k), :])
-            part = slice(k * PAIR, (k + 1) * PAIR)
-            nc.sync.dma_start(out=a_rows[:, part, :], in_=a_view[:, part, :])
         w_rows = weights.tile([P, OUT_TILES, FEATURES * KNOTS], BF16)
-        nc.sync.dma_start(out=w_rows[:], in_=spline_weight.rearrange("(c p) i g -> p c (i g)", p=P))
-        for k in range(2, len(ROUNDS)):
+        for k in range(len(ROUNDS)):
             if opens(k):
                 nc.sync.dma_start(out=x_rows[:, rows_of(k), :], in_=x_view[:, rows_of(k), :])
+            if k < OUT_TILES // PAIR:
+                part = slice(k * PAIR, (k + 1) * PAIR)
+                nc.sync.dma_start(out=a_rows[:, part, :], in_=a_view[:, part, :])
+            if k == OUT_TILES // PAIR:
+                nc.sync.dma_start(out=w_rows[:], in_=spline_weight.rearrange("(c p) i g -> p c (i g)", p=P))
 
         identity = consts.tile([P, P], F32)
         make_identity(nc, identity[:])
@@ -281,7 +281,7 @@ def tile_advancedkanlayer_pa_t_kernel(tc, x_norm, spline_weight, base_activation
             count = len(tiles_of(k))
             if k not in inner:
                 inner[k] = twice.tile([P, PACK * words_of(k)], BF16, name="inner")
-            for t in tiles:
+            for t in range(count)[tiles]:
                 first = (h * count + t) * P * PACK
                 place = inner[k][:, first : first + P * PACK].rearrange("p (r b) -> p r b", b=PACK)
                 source = sums[k, t, h][:].rearrange("p b r -> p r b")
@@ -432,7 +432,7 @@ def tile_advancedkanlayer_pa_t_kernel(tc, x_norm, spline_weight, base_activation
         minus_half_knots = consts.tile([P, KNOTS], F32)
         nc.vector.tensor_scalar_mul(out=minus_half_knots[:], in0=spread[:, 0, :KNOTS], scalar1=-0.5)
         turn_x(1)
-        group_x(0, nc.scalar.copy)
+        group_x(0, nc.vector.tensor_copy)
         group_x(1, nc.vector.tensor_copy)
         distances(0)
         squares(0)
@@ -443,15 +443,15 @@ def tile_advancedkanlayer_pa_t_kernel(tc, x_norm, spline_weight, base_activation
 
         for s in range(len(ROUNDS) + 2):
             distances(s + 1)
-            leave(s - 1, 0, (0, 1))
+            leave(s - 1, 0, slice(0, 2))
             group_x(s + 2, nc.scalar.copy)
             squares(s + 1)
             cubes(s)
-            leave(s - 1, 1, (0,))
+            leave(s - 1, 1, slice(0, 1))
             if s - 1 not in SUMMED:
                 choose(s - 1)
             inners(s)
-            leave(s - 1, 1, (1,))
+            leave(s - 1, 1, slice(1, 2))
             if s - 1 not in SUMMED:
                 quantise_basis(s - 1)
             outers(s)

import math
from contextlib import ExitStack

import concourse.mybir as mybir
from concourse.masks import make_identity

F32 = mybir.dt.float32
BF16 = mybir.dt.bfloat16
U32 = mybir.dt.uint32
U8 = mybir.dt.uint8
FP8X4 = mybir.dt.float8_e4m3fn_x4
ALU = mybir.AluOpType
ACT = mybir.ActivationFunctionType

P = 128
PACK = 4
BATCH, FEATURES, OUTPUTS, KNOTS = 4096, 512, 512, 2
FLOPS = 2 * BATCH * OUTPUTS * (FEATURES * KNOTS + FEATURES)

ROW_TILES = BATCH // P
OUT_TILES = OUTPUTS // P
PAIR = 2
HALVES = 2
ROUNDS = (
    [(0, 1, 0, HALVES), (1, 1, 0, HALVES)]
    + [(t, PAIR, 0, HALVES) for t in range(PAIR, ROW_TILES - PAIR, PAIR)]
    + [(ROW_TILES - 2, 1, 0, HALVES), (ROW_TILES - 1, 1, 0, 1), (ROW_TILES - 1, 1, 1, 1)]
)
SUMMED = [k for k in range(len(ROUNDS) - 3) if k < 2 or k % 3 != 0]
VECTOR_FINISHES = 10
TILE_GROUPED = P * PACK

LAST_FACTOR = 0.1
SPLINE_FACTORS = (1.0, 4.0)
BASE_FACTORS = (1.0,)

ROOT_SIX = math.sqrt(6.0)


def turn_rows(nc, turned, identity, rows, tiles):
    for h in range(HALVES):
        for t in range(tiles):
            nc.tensor.transpose(
                out=turned[:, h, t * P : (t + 1) * P],
                in_=rows[:, t, :].bitcast(F32)[:, h * P : (h + 1) * P],
                identity=identity,
            )


def group_words(copy, grouped, turned):
    copy(
        out=grouped.bitcast(F32).rearrange("p (r h) -> p r h", h=HALVES),
        in_=turned[:].rearrange("p h r -> p r h"),
    )


def tile_advancedkanlayer_pa_t_kernel(tc, x_norm, spline_weight, base_activation, grid_points, out):
    nc = tc.nc
    with ExitStack() as stack:
        consts = stack.enter_context(tc.tile_pool(name="consts", bufs=1))
        weights = stack.enter_context(tc.tile_pool(name="weights", bufs=1))
        twice = stack.enter_context(tc.tile_pool(name="twice", bufs=2))
        thrice = stack.enter_context(tc.tile_pool(name="thrice", bufs=3))
        bank_psum = stack.enter_context(tc.psum_pool(name="bank_psum", bufs=6))
        acc_psum = stack.enter_context(tc.psum_pool(name="acc_psum", bufs=PAIR))
        stack.enter_context(tc.manual_schedule())

        def tiles_of(k):
            first, count = ROUNDS[k][:2]
            return range(first, first + count)

        def rows_of(k):
            return slice(tiles_of(k).start, tiles_of(k).stop)

        def halves_of(k):
            first, count = ROUNDS[k][2:]
            return range(first, first + count)

        def opens(k):
            return halves_of(k).start == 0

        def closes(k):
            return halves_of(k).stop == HALVES

        def words_of(k):
            return len(halves_of(k)) * len(tiles_of(k)) * P

        x_view = x_norm.rearrange("(p t) i -> p t i", t=ROW_TILES)
        out_view = out.rearrange("(p t) o -> p t o", t=ROW_TILES)

        knots = consts.tile([P, KNOTS], BF16)
        nc.vector.memset(knots[:], 0.0)
        nc.scalar.dma_start(out=knots[:1, :], in_=grid_points.rearrange("(o g) -> o g", o=1))
        x_rows = consts.tile([P, ROW_TILES, FEATURES], BF16)
        a_rows = weights.tile([P, OUT_TILES, FEATURES], BF16)
        a_view = base_activation.rearrange("(c p) i -> p c i", p=P)
        w_rows = weights.tile([P, OUT_TILES, FEATURES * KNOTS], BF16)
        for k in range(len(ROUNDS)):
            if opens(k):
                nc.sync.dma_start(out=x_rows[:, rows_of(k), :], in_=x_view[:, rows_of(k), :])
            if k < OUT_TILES // PAIR:
                part = slice(k * PAIR, (k + 1) * PAIR)
                nc.sync.dma_start(out=a_rows[:, part, :], in_=a_view[:, part, :])
            if k == OUT_TILES // PAIR:
                nc.sync.dma_start(out=w_rows[:], in_=spline_weight.rearrange("(c p) i g -> p c (i g)", p=P))

        identity = consts.tile([P, P], F32)
        make_identity(nc, identity[:])
        ones = consts.tile([P, P], BF16)
        nc.vector.memset(ones[:], 1.0)
        minus_one = consts.tile([P, 1], F32)
        nc.vector.memset(minus_one[:], -1.0)
        minus_ten = consts.tile([P, 1], F32)
        nc.vector.memset(minus_ten[:], -10.0)
        outer_bias = consts.tile([P, 1], F32)
        nc.vector.tensor_scalar_mul(out=outer_bias[:], in0=minus_one[:], scalar1=ROOT_SIX)
        mixed_bias = consts.tile([P, 1], F32)
        nc.vector.tensor_scalar_mul(out=mixed_bias[:], in0=minus_one[:], scalar1=1.5 * ROOT_SIX)

        turned_x, x_grouped, x_codes, x_scales = {}, {}, {}, {}
        dist, outer_sq, mixed_sq, cube, inner, outer, basis = {}, {}, {}, {}, {}, {}, {}
        basis_codes, basis_scales, acc, result = {}, {}, {}, {}
        sums, turned_outer = {}, {}

        def by_feature(tile):
            return tile[:].rearrange("p g c -> p c g")

        def live(k):
            return 0 <= k < len(ROUNDS)

        def turn_x(k):
            if not live(k):
                return
            if not opens(k):
                turned_x[k] = turned_x[k - 1]
                return
            count = len(tiles_of(k))
            turned_x[k] = bank_psum.tile([P, HALVES, count * P], F32, name="bank")
            turn_rows(nc, turned_x[k], identity[:], x_rows[:, rows_of(k), :], count)

        def group_x(k, copy):
            if not live(k):
                return
            if not opens(k):
                x_grouped[k] = x_grouped[k - 1]
                return
            x_grouped[k] = thrice.tile([P, len(tiles_of(k)) * TILE_GROUPED], BF16, align_bytes=64, name="x_grouped")
            group_words(copy, x_grouped[k][:], turned_x[k])

        def distances(k):
            if not live(k):
                return
            if k in SUMMED:
                dist[k] = thrice.tile([P, KNOTS, len(tiles_of(k)) * FEATURES], F32, name="dist")
                for g in range(KNOTS):
                    nc.scalar.activation(
                        out=dist[k][:, g, :].rearrange("r (b e p) -> r b e p", e=2, p=P),
                        in_=x_rows[:, rows_of(k), :].rearrange("r t (h p e) -> r (t h) e p", h=HALVES, e=2),
                        func=ACT.Abs,
                        bias=minus_half_knots[:, g : g + 1],
                        scale=0.5,
                    )
                return
            rows = len(tiles_of(k)) * P
            dist[k] = thrice.tile([P, KNOTS, len(halves_of(k)) * rows * 2], F32, name="dist")
            words = x_grouped[k][:].rearrange("p (r h e) -> p h r e", h=HALVES, e=2)
            for g in range(KNOTS):
                nc.scalar.activation(
                    out=dist[k][:, g, :].rearrange("p (h r e) -> p h r e", r=rows, e=2),
                    in_=words[:, halves_of(k).start : halves_of(k).stop],
                    func=ACT.Abs,
                    bias=minus_two_knots[:, g : g + 1],
                    scale=2.0,
                )

        def squares(k):
            if not live(k):
                return
            features = 2 * words_of(k)
            if k in SUMMED:
                outer_sq[k] = thrice.tile([P, KNOTS, features], F32, name="outer_sq")
                nc.scalar.activation(
                    out=outer_sq[k][:], in_=dist[k][:], func=ACT.Square, bias=minus_one[:], scale=2.0
                )
                return
            outer_sq[k] = thrice.tile([P, features, KNOTS], F32, name="outer_sq")
            nc.scalar.activation(
                out=outer_sq[k][:], in_=by_feature(dist[k]), func=ACT.Square, bias=outer_bias[:], scale=0.5 * ROOT_SIX
            )
            mixed_sq[k] = thrice.tile([P, features, KNOTS], F32, name="mixed_sq")
            nc.scalar.activation(
                out=mixed_sq[k][:], in_=by_feature(dist[k]), func=ACT.Square, bias=mixed_bias[:], scale=ROOT_SIX
            )

        def quantise_x(k):
            if not live(k) or not opens(k):
                return
            rows = len(tiles_of(k)) * P
            x_codes[k] = thrice.tile([P, rows], U32, align_bytes=64, name="x_codes")
            x_scales[k] = thrice.tile([P, rows], U8, align_bytes=64, name="x_scales")
            nc.vector.quantize_mx(out=x_codes[k][:].bitcast(FP8X4), scales=x_scales[k][:], in_=x_grouped[k][:])

        def cubes(k):
            if not live(k):
                return
            if k in SUMMED:
                cube[k] = twice.tile([P, KNOTS, 2 * words_of(k)], F32, name="cube")
                nc.vector.scalar_tensor_tensor(
                    out=cube[k][:], in0=dist[k][:], scalar=0.5, in1=outer_sq[k][:], op0=ALU.subtract, op1=ALU.mult
                )
                return
            cube[k] = twice.tile([P, 2 * words_of(k), KNOTS], F32, name="cube")
            nc.vector.scalar_tensor_tensor(
                out=cube[k][:], in0=by_feature(dist[k]), scalar=2.0, in1=outer_sq[k][:], op0=ALU.subtract, op1=ALU.mult
            )

        def inners(k):
            if not live(k):
                return
            if k in SUMMED:
                return
            inner[k] = twice.tile([P, 2 * words_of(k), KNOTS], BF16, name="inner")
            nc.vector.scalar_tensor_tensor(
                out=inner[k][:], in0=mixed_sq[k][:], scalar=0.5, in1=cube[k][:], op0=ALU.add, op1=ALU.add
            )

        def outers(k):
            if not live(k):
                return
            outer[k] = twice.tile([P, 2 * words_of(k), KNOTS], BF16, name="outer")
            if k in SUMMED:
                nc.vector.tensor_scalar(
                    out=outer[k][:], in0=by_feature(cube[k]), scalar1=-8.0, scalar2=0.0, op0=ALU.mult, op1=ALU.max
                )
                return
            if not (opens(k) and closes(k)):
                nc.scalar.activation(out=outer[k][:], in_=cube[k][:], func=ACT.Relu, scale=-1.0 / 3.0)
                return
            nc.vector.tensor_scalar(
                out=outer[k][:], in0=cube[k][:], scalar1=-1.0 / 3.0, scalar2=0.0, op0=ALU.mult, op1=ALU.max
            )

        def block(tile, k, t, h, e):
            first = ((t * HALVES + h) * 2 + e) * P
            return tile[:, first : first + P]

        def sum_terms(k):
            if not live(k) or k not in SUMMED:
                return
            for t in range(len(tiles_of(k))):
                for h in range(HALVES):
                    sums[k, t, h] = bank_psum.tile([P, PACK, P], F32, name="bank")
                    for e in range(2):
                        for g in range(KNOTS):
                            terms = [outer_sq[k], dist[k], cube[k]]
                            for n, term in enumerate(terms):
                                nc.tensor.matmul(
                                    out=sums[k, t, h][:, 2 * e + g, :],
                                    lhsT=block(term[:, g, :], k, t, h, e),
                                    rhs=identity[:],
                                    is_transpose=True,
                                    start=(n == 0),
                                    stop=(n == len(terms) - 1),
                                )

        def turn_outer(k):
            if not live(k) or k not in SUMMED:
                return
            for t in range(len(tiles_of(k))):
                turned_outer[k, t] = bank_psum.tile([P, HALVES, P, 2], F32, name="bank")
                words = outer[k][:].rearrange("r c g -> r (c g)").bitcast(F32)
                for h in range(HALVES):
                    for e in range(2):
                        nc.tensor.transpose(
                            out=turned_outer[k, t][:, h, :, e], in_=block(words, k, t, h, e), identity=identity[:]
                        )

        def leave(k, h, tiles):
            if not live(k) or k not in SUMMED:
                return
            count = len(tiles_of(k))
            if k not in inner:
                inner[k] = twice.tile([P, PACK * words_of(k)], BF16, name="inner")
            for t in range(count)[tiles]:
                first = (h * count + t) * P * PACK
                place = inner[k][:, first : first + P * PACK].rearrange("p (r b) -> p r b", b=PACK)
                source = sums[k, t, h][:].rearrange("p b r -> p r b")
                if h == 0:
                    nc.scalar.activation(out=place, in_=source, func=ACT.Identity, bias=minus_ten[:], scale=24.0)
                else:
                    nc.vector.tensor_scalar(
                        out=place, in0=source, scalar1=24.0, scalar2=-10.0, op0=ALU.mult, op1=ALU.add
                    )

        def choose(k):
            if not live(k):
                return
            basis[k] = twice.tile([P, PACK * words_of(k)], BF16, align_bytes=64, name="basis")
            if k in SUMMED:
                count = len(tiles_of(k))
                for t in range(count):
                    nc.vector.tensor_tensor(
                        out=basis[k][:].rearrange("p (h t c) -> p t h c", h=HALVES, t=count)[:, t],
                        in0=inner[k][:].rearrange("p (h t c) -> p t h c", h=HALVES, t=count)[:, t],
                        in1=turned_outer[k, t][:].rearrange("p h r e -> p h (r e)").bitcast(BF16),
                        op=ALU.min,
                    )
                return
            nc.vector.tensor_tensor(
                out=basis[k][:],
                in0=inner[k][:].rearrange("p c g -> p (c g)"),
                in1=outer[k][:].rearrange("p c g -> p (c g)"),
                op=ALU.min,
            )

        def quantise_basis(k):
            if not live(k):
                return
            basis_codes[k] = twice.tile([P, words_of(k)], U32, align_bytes=64, name="basis_codes")
            basis_scales[k] = twice.tile([P, words_of(k)], U8, align_bytes=64, name="basis_scales")
            nc.vector.quantize_mx(
                out=basis_codes[k][:].bitcast(FP8X4), scales=basis_scales[k][:], in_=basis[k][:]
            )

        def groups_of(tile):
            width = OUTPUTS // 2 if tile == ROW_TILES - 1 else OUTPUTS
            return [slice(first, first + width) for first in range(0, OUTPUTS, width)]

        def products(k):
            if not live(k):
                return
            for t, tile in enumerate(tiles_of(k)):
                passes = []
                if opens(k):
                    for outputs in groups_of(tile):
                        acc[tile, outputs.start] = acc_psum.tile([P, OUTPUTS], F32, name="acc")
                    cols = slice(t * P, (t + 1) * P)
                    for moving in base_weights:
                        passes.append((x_codes[k][:, cols], x_scales[k][:, cols], moving))
                for h in halves_of(k):
                    first = ((h - halves_of(k).start) * len(tiles_of(k)) + t) * P
                    cols = slice(first, first + P)
                    for moving in spline_weights[h]:
                        passes.append((basis_codes[k][:, cols], basis_scales[k][:, cols], moving))
                for outputs in groups_of(tile):
                    for n, (codes, scales, moving) in enumerate(passes):
                        nc.tensor.matmul_mx(
                            out=acc[tile, outputs.start][:, : outputs.stop - outputs.start],
                            lhsT=codes.bitcast(FP8X4),
                            lhsT_scale=scales,
                            rhs=moving[0][:, outputs].bitcast(FP8X4),
                            rhs_scale=moving[1][:, outputs],
                            start=(opens(k) and n == 0),
                            stop=(closes(k) and n == len(passes) - 1),
                        )

        def finish(k, part):
            if not live(k) or not closes(k):
                return
            first = tiles_of(k).start
            if first == ROW_TILES - 1:
                if part == "vector":
                    return
                for n, outputs in enumerate(groups_of(first)):
                    columns = acc[first, outputs.start][:, : outputs.stop - outputs.start]
                    half = thrice.tile([P, outputs.stop - outputs.start], F32, name="half%d" % n)
                    if n == 0:
                        nc.scalar.activation(out=half[:], in_=columns, func=ACT.Copy, scale=LAST_FACTOR)
                        nc.scalar.dma_start(out=out_view[:, first, outputs], in_=half[:])
                    else:
                        nc.vector.tensor_scalar_mul(out=half[:], in0=columns, scalar1=LAST_FACTOR)
                        nc.sync.dma_start(out=out_view[:, first, outputs], in_=half[:])
                return
            if part == "scalar":
                result[k] = thrice.tile([P, len(tiles_of(k)), OUTPUTS], F32, name="result")
            for t, tile in enumerate(tiles_of(k)):
                on_vector = tile % VECTOR_FINISHES == VECTOR_FINISHES // 2
                if part == "vector" and on_vector:
                    nc.vector.tensor_scalar_mul(out=result[k][:, t, :], in0=acc[tile, 0][:], scalar1=LAST_FACTOR)
                if part == "scalar" and not on_vector:
                    nc.scalar.activation(out=result[k][:, t, :], in_=acc[tile, 0][:], func=ACT.Copy, scale=LAST_FACTOR)
            if part == "vector":
                nc.sync.dma_start(out=out_view[:, rows_of(k), :], in_=result[k][:])

        def turn_base(turned, c, t):
            turn_rows(nc, turned[:, :, t * P : (t + 1) * P], identity[:], a_rows[:, c : c + 1, :], 1)

        def turn_spline(h):
            def turn(turned, c, t):
                for e in range(2):
                    nc.tensor.transpose(
                        out=turned[:, e, t * P : (t + 1) * P],
                        in_=w_rows[:, c, :].bitcast(F32)[:, 2 * P * h + e : 2 * P * (h + 1) : 2],
                        identity=identity[:],
                    )

            return turn

        def group_weight(copy, turn):
            grouped = twice.tile([P, OUTPUTS * PACK], BF16, align_bytes=64, name="w_grouped")
            for pair in range(OUT_TILES // PAIR):
                turned_w = bank_psum.tile([P, HALVES, PAIR * P], F32, name="bank")
                for t in range(PAIR):
                    turn(turned_w, pair * PAIR + t, t)
                columns = slice(pair * PAIR * TILE_GROUPED, (pair + 1) * PAIR * TILE_GROUPED)
                group_words(copy, grouped[:, columns], turned_w)
            return grouped

        def quantise_weight(label, grouped, factors):
            operands = []
            for n, factor in enumerate(factors):
                scaled = grouped
                if factor != 1.0:
                    scaled = twice.tile([P, OUTPUTS * PACK], BF16, align_bytes=64, name="w_scaled")
                    nc.vector.tensor_scalar_mul(out=scaled[:], in0=grouped[:], scalar1=factor)
                codes = weights.tile([P, OUTPUTS], U32, align_bytes=64, name="%s_codes%d" % (label, n))
                scales = weights.tile([P, OUTPUTS], U8, align_bytes=64, name="%s_scales%d" % (label, n))
                nc.vector.quantize_mx(out=codes[:].bitcast(FP8X4), scales=scales[:], in_=scaled[:])
                operands.append((codes, scales))
            return operands

        def make_spline(h):
            return quantise_weight("spline%d" % h, group_weight(nc.vector.tensor_copy, turn_spline(h)), SPLINE_FACTORS)

        spline_weights = {}

        turn_x(0)
        spread = bank_psum.tile([P, HALVES, PAIR * P], F32, name="bank")
        nc.tensor.matmul(out=spread[:, 0, :KNOTS], lhsT=ones[:], rhs=knots[:], start=True, stop=True)
        minus_two_knots = consts.tile([P, KNOTS], F32)
        nc.vector.tensor_scalar_mul(out=minus_two_knots[:], in0=spread[:, 0, :KNOTS], scalar1=-2.0)
        minus_half_knots = consts.tile([P, KNOTS], F32)
        nc.vector.tensor_scalar_mul(out=minus_half_knots[:], in0=spread[:, 0, :KNOTS], scalar1=-0.5)
        turn_x(1)
        group_x(0, nc.vector.tensor_copy)
        group_x(1, nc.vector.tensor_copy)
        distances(0)
        squares(0)
        base_grouped = group_weight(nc.vector.tensor_copy, turn_base)
        base_weights = quantise_weight("base", base_grouped, BASE_FACTORS)
        quantise_x(0)
        turn_x(2)

        for s in range(len(ROUNDS) + 2):
            distances(s + 1)
            leave(s - 1, 0, slice(0, 2))
            group_x(s + 2, nc.scalar.copy)
            squares(s + 1)
            cubes(s)
            leave(s - 1, 1, slice(0, 1))
            if s - 1 not in SUMMED:
                choose(s - 1)
            inners(s)
            leave(s - 1, 1, slice(1, 2))
            if s - 1 not in SUMMED:
                quantise_basis(s - 1)
            outers(s)
            if s - 1 in SUMMED:
                choose(s - 1)
            finish(s - 2, "scalar")
            if s < HALVES:
                spline_weights[s] = make_spline(s)
            turn_x(s + 3)
            quantise_x(s + 1)
            if s - 1 in SUMMED:
                quantise_basis(s - 1)
            sum_terms(s)
            turn_outer(s)
            products(s - 1)
            finish(s - 2, "vector")
